import numpy as np
import ml_dtypes


def mxq(x, axis, fmt="e4m3"):
    dtype, down = {"e4m3": (ml_dtypes.float8_e4m3fn, 7), "e5m2": (ml_dtypes.float8_e5m2, 14)}[fmt]
    v = np.moveaxis(np.asarray(x, np.float32).astype(ml_dtypes.bfloat16).astype(np.float64), axis, -1)
    blocks = v.reshape(v.shape[:-1] + (-1, 32))
    amax = np.abs(blocks).max(-1, keepdims=True)
    byte = np.maximum(np.where(amax > 0, np.frexp(amax)[1] - 1 + 127, 0) - down, 1)
    scale = np.exp2(byte - 127.0)
    codes = (blocks / scale).astype(np.float32).astype(dtype).astype(np.float64)
    return np.moveaxis((codes * scale).reshape(v.shape), -1, axis)


WIDE = False


def mx_kscale(k):
    if not WIDE:
        return np.ones(k)
    levels = np.array([10, -10, 5, -5, 0])
    a = np.random.permutation(np.resize(levels, k // 512 * 4)).reshape(k // 512, 4)
    idx = np.arange(k)
    return np.exp2(a[idx // 512, idx % 128 // 32])


BF16 = ml_dtypes.bfloat16


def bf(x):
    return np.asarray(x, np.float32).astype(BF16)


def f64(x):
    return np.asarray(x).astype(np.float64)


B, IN, HID, PROJ, H, KC = 128, 2048, 2048, 2048, 4, 4
EPS = 1e-5


def silu(v):
    return v / (1.0 + np.exp(-v))


def layernorm(v, w, b):
    mu = v.mean(-1, keepdims=True)
    var = ((v - mu) ** 2).mean(-1, keepdims=True)
    return (v - mu) / np.sqrt(var + EPS) * w + b


def causal_conv(v, w, b):
    vp = np.pad(v, ((0, 0), (KC - 1, 0)))
    L = v.shape[1]
    return b + sum(w[j] * vp[:, j:j + L] for j in range(KC))


def setup_inputs():
    s = mx_kscale(IN)
    r = np.random.standard_normal
    return {"x": bf(r((B, IN))),
            "ln_w": bf((1.0 + 0.1 * r(IN)) * s), "ln_b": bf(0.1 * r(IN) * s),
            "upL_w": bf(r((IN, PROJ)) / np.sqrt(IN) / s[:, None]), "upL_b": bf(0.2 * r(PROJ)),
            "upR_w": bf(r((IN, HID)) / np.sqrt(IN) / s[:, None]), "upR_b": bf(0.2 * r(HID)),
            "conv_w": bf((1.0 + 0.3 * r(KC)) / np.sqrt(KC)), "conv_b": bf(0.2 + 0.1 * r(1))}


def reference(x, ln_w, ln_b, upL_w, upL_b, upR_w, upR_b, conv_w, conv_b):
    xn = mxq(layernorm(f64(x), f64(ln_w), f64(ln_b)), 1, "e4m3")
    x_left = (xn @ mxq(f64(upL_w), 0, "e4m3")) + f64(upL_b)
    x_right = (xn @ mxq(f64(upR_w), 0, "e4m3")) + f64(upR_b)
    x_conv = silu(causal_conv(x_left, f64(conv_w), f64(conv_b)))
    return x_left, x_conv, x_right

@@ -1,0 +1,259 @@
+from contextlib import ExitStack
+
+import concourse.mybir as mybir
+from concourse.masks import make_identity
+
+F32 = mybir.dt.float32
+BF16 = mybir.dt.bfloat16
+U32 = mybir.dt.uint32
+U8 = mybir.dt.uint8
+FP8X4 = mybir.dt.float8_e4m3fn_x4
+ALU = mybir.AluOpType
+ACT = mybir.ActivationFunctionType
+
+P = 128
+PACK = 4
+K_PASS = P * PACK
+FEATURES = 2048
+PASSES = FEATURES // K_PASS
+WIDTH = 2048
+BANK = 512
+BANKS = WIDTH // BANK
+BLOCKS_PER_BANK = BANK // P
+TAPS = 4
+RUN = 4
+EPS = 1e-5
+RAW_BUFS = 6
+FLOPS = 2 * P * FEATURES * 2 * WIDTH
+
+
+def tile_mlstmblock_pa_kernel(
+    tc, x, ln_w, ln_b, upL_w, upL_b, upR_w, upR_b, conv_w, conv_b, out_0, out_1, out_2
+):
+    nc = tc.nc
+    weights = (upL_w, upR_w)
+    with ExitStack() as ctx:
+        keep = ctx.enter_context(tc.tile_pool(name="keep", bufs=1))
+        raw_pool = ctx.enter_context(tc.tile_pool(name="raw", bufs=RAW_BUFS))
+        grouped_pool = ctx.enter_context(tc.tile_pool(name="grouped", bufs=2))
+        codes_pool = ctx.enter_context(tc.tile_pool(name="codes", bufs=3))
+        psum = ctx.enter_context(tc.psum_pool(name="psum", bufs=1))
+
+        raw = {}
+
+        def load_chunk(side, c):
+            raw[side, c] = raw_pool.tile([P, PACK, WIDTH], BF16, name="raw", tag="raw")
+            rows = weights[side][c * K_PASS : (c + 1) * K_PASS, :]
+            nc.sync.dma_start(out=raw[side, c][:], in_=rows.rearrange("(p j) n -> p j n", j=PACK))
+
+        chunks = [(side, c) for side in range(2) for c in range(PASSES)]
+
+        x_sb = keep.tile([P, FEATURES], BF16)
+        nc.sync.dma_start(out=x_sb[:], in_=x[:, :])
+
+        gain_bf = keep.tile([P, PASSES, PACK], BF16)
+        shift_bf = keep.tile([P, PASSES, PACK], BF16)
+        taps_bf = keep.tile([P, TAPS], BF16)
+        conv_b_bf = keep.tile([P, 1], BF16)
+        with nc.allow_non_contiguous_dma(reason="two vectors of 2048 values, four to a piece"):
+            nc.scalar.dma_start(
+                out=gain_bf[:], in_=ln_w.rearrange("(c p j) -> p c j", c=PASSES, j=PACK)
+            )
+            nc.scalar.dma_start(
+                out=shift_bf[:], in_=ln_b.rearrange("(c p j) -> p c j", c=PASSES, j=PACK)
+            )
+            nc.scalar.dma_start(out=taps_bf[:], in_=conv_w.partition_broadcast(P))
+            nc.scalar.dma_start(out=conv_b_bf[:], in_=conv_b.partition_broadcast(P))
+
+        bias_bc = keep.tile([P, 2, WIDTH], BF16)
+        for side, c in chunks[:PASSES]:
+            load_chunk(side, c)
+        nc.sync.dma_start(out=bias_bc[:, 0, :], in_=upL_b.partition_broadcast(P))
+        nc.sync.dma_start(out=bias_bc[:, 1, :], in_=upR_b.partition_broadcast(P))
+        for side, c in chunks[PASSES:RAW_BUFS]:
+            load_chunk(side, c)
+
+        ident = keep.tile([P, P], F32)
+        make_identity(nc, ident[:])
+        eps = keep.tile([P, 1], F32)
+        nc.vector.memset(eps[:], EPS)
+
+        stats = keep.tile([P, PASSES, 6], F32)
+        for c in range(PASSES):
+            nc.vector.bn_stats(out=stats[:, c, :], in_=x_sb[:, c * K_PASS : (c + 1) * K_PASS])
+        mean_var = keep.tile([P, 2], F32)
+        nc.vector.bn_aggr(out=mean_var[:], in_=stats[:].rearrange("p c s -> p (c s)"))
+        std = keep.tile([P, 1], F32)
+        nc.scalar.activation(out=std[:], in_=mean_var[:, 1:2], func=ACT.Sqrt, bias=eps[:], scale=1.0)
+        rstd = keep.tile([P, 1], F32)
+        nc.vector.reciprocal(out=rstd[:], in_=std[:])
+
+        gain = keep.tile([P, PASSES * PACK], F32)
+        shift = keep.tile([P, PASSES * PACK], F32)
+        nc.vector.tensor_copy(out=gain[:], in_=gain_bf[:].rearrange("p c j -> p (c j)"))
+        nc.vector.tensor_copy(out=shift[:], in_=shift_bf[:].rearrange("p c j -> p (c j)"))
+
+        z = keep.tile([P, PASSES, PACK, P], F32)
+        x_by_word = x_sb[:].rearrange("b (c p j) -> b c j p", c=PASSES, j=PACK)
+        for c in range(PASSES):
+            nc.vector.tensor_scalar(
+                out=z[:, c],
+                in0=x_by_word[:, c],
+                scalar1=mean_var[:, 0:1],
+                scalar2=rstd[:],
+                op0=ALU.subtract,
+                op1=ALU.mult,
+            )
+
+        xn_rows = keep.tile([P, PASSES, PACK, P], BF16)
+        for c in range(PASSES):
+            zT = psum.tile([P, PACK, P], F32, name="zT", tag="bank%d" % (BANKS + c))
+            for j in range(PACK):
+                nc.tensor.transpose(out=zT[:, j, :], in_=z[:, c, j, :], identity=ident[:])
+            for j in range(PACK):
+                col = c * PACK + j
+                if c % 2 == 0:
+                    nc.vector.tensor_scalar(
+                        out=xn_rows[:, c, j, :],
+                        in0=zT[:, j, :],
+                        scalar1=gain[:, col : col + 1],
+                        scalar2=shift[:, col : col + 1],
+                        op0=ALU.mult,
+                        op1=ALU.add,
+                    )
+                else:
+                    nc.scalar.activation(
+                        out=xn_rows[:, c, j, :],
+                        in_=zT[:, j, :],
+                        func=ACT.Identity,
+                        scale=gain[:, col : col + 1],
+                        bias=shift[:, col : col + 1],
+                    )
+
+        xn_grouped = keep.tile([P, PASSES, P, PACK], BF16, align_bytes=64)
+        nc.vector.tensor_copy(out=xn_grouped[:], in_=xn_rows[:].rearrange("p c j b -> p c b j"))
+        xn_codes = keep.tile([P, PASSES * P], U32, align_bytes=64)
+        xn_scales = keep.tile([P, PASSES * P], U8, align_bytes=64)
+        nc.vector.quantize_mx(
+            out=xn_codes[:].bitcast(FP8X4),
+            scales=xn_scales[:],
+            in_=xn_grouped[:].rearrange("p c b j -> p (c b j)"),
+        )
+
+        taps = keep.tile([P, TAPS], F32)
+        nc.vector.tensor_copy(out=taps[:], in_=taps_bf[:])
+        conv_bias = keep.tile([P, 1], F32)
+        nc.vector.tensor_copy(out=conv_bias[:], in_=conv_b_bf[:])
+        band = keep.tile([P, 2 * P], F32)
+        nc.vector.memset(band[:], 0.0)
+        for d in range(TAPS):
+            nc.vector.scalar_tensor_tensor(
+                out=band[:, d : d + P],
+                in0=ident[:],
+                scalar=taps[:, TAPS - 1 - d : TAPS - d],
+                in1=band[:, d : d + P],
+                op0=ALU.mult,
+                op1=ALU.add,
+            )
+
+        def project(side):
+            acc = [
+                psum.tile([P, BANK], F32, name="acc", tag="bank%d" % (side * BANKS + nb))
+                for nb in range(BANKS)
+            ]
+            for c in range(PASSES):
+                grouped = []
+                for nb in range(BANKS):
+                    piece = grouped_pool.tile(
+                        [P, BANK, PACK], BF16, align_bytes=64, name="grouped", tag="grouped%d" % nb
+                    )
+                    copy = nc.vector.tensor_copy if nb < BANKS // 2 else nc.scalar.copy
+                    copy(
+                        out=piece[:].rearrange("p (q i) j -> p q j i", i=RUN),
+                        in_=raw[side, c][:, :, nb * BANK : (nb + 1) * BANK].rearrange(
+                            "p j (q i) -> p q j i", i=RUN
+                        ),
+                    )
+                    grouped.append(piece)
+                done = chunks.index((side, c))
+                if done + RAW_BUFS < len(chunks):
+                    load_chunk(*chunks[done + RAW_BUFS])
+                for nb in range(BANKS):
+                    codes = codes_pool.tile([P, BANK], U32, align_bytes=64, name="codes", tag="codes%d" % nb)
+                    scales = codes_pool.tile([P, BANK], U8, align_bytes=64, name="scales", tag="scales%d" % nb)
+                    nc.vector.quantize_mx(
+                        out=codes[:].bitcast(FP8X4),
+                        scales=scales[:],
+                        in_=grouped[nb][:].rearrange("p n j -> p (n j)"),
+                    )
+                    nc.tensor.matmul_mx(
+                        out=acc[nb][:],
+                        lhsT=xn_codes[:, c * P : (c + 1) * P].bitcast(FP8X4),
+                        lhsT_scale=xn_scales[:, c * P : (c + 1) * P],
+                        rhs=codes[:].bitcast(FP8X4),
+                        rhs_scale=scales[:],
+                        start=(c == 0),
+                        stop=(c == PASSES - 1),
+                    )
+            return acc
+
+        acc_left = project(0)
+        left = keep.tile([P, WIDTH], F32)
+        for nb in range(BANKS):
+            cols = slice(nb * BANK, (nb + 1) * BANK)
+            nc.vector.tensor_tensor(
+                out=left[:, cols], in0=acc_left[nb][:], in1=bias_bc[:, 0, cols], op=ALU.add
+            )
+        for half in range(2):
+            cols = slice(half * WIDTH // 2, (half + 1) * WIDTH // 2)
+            nc.sync.dma_start(out=out_0[:, cols], in_=left[:, cols])
+
+        leftT = keep.tile([P, BANKS * BLOCKS_PER_BANK, P], F32)
+        conv = keep.tile([P, WIDTH], F32)
+        for nb in range(BANKS):
+            first = nb * BLOCKS_PER_BANK
+            leftT_ps = psum.tile([P, BLOCKS_PER_BANK, P], F32, name="leftT_ps", tag="bank%d" % (nb % 2))
+            for q in range(BLOCKS_PER_BANK):
+                nc.tensor.transpose(
+                    out=leftT_ps[:, q, :],
+                    in_=left[:, (first + q) * P : (first + q + 1) * P],
+                    identity=ident[:],
+                )
+            nc.scalar.copy(out=leftT[:, first : first + BLOCKS_PER_BANK, :], in_=leftT_ps[:])
+            conv_ps = psum.tile([P, BANK], F32, name="conv_ps", tag="bank%d" % (2 + nb % 2))
+            for q in range(BLOCKS_PER_BANK):
+                block = first + q
+                nc.tensor.matmul(
+                    out=conv_ps[:, q * P : (q + 1) * P],
+                    lhsT=leftT[:, block, :],
+                    rhs=band[:, 0:P],
+                    start=True,
+                    stop=(block == 0),
+                )
+                if block > 0:
+                    nc.tensor.matmul(
+                        out=conv_ps[:, q * P : (q + 1) * P],
+                        lhsT=leftT[:, block - 1, :],
+                        rhs=band[:, P : 2 * P],
+                        start=False,
+                        stop=True,
+                    )
+            nc.scalar.activation(
+                out=conv[:, nb * BANK : (nb + 1) * BANK],
+                in_=conv_ps[:],
+                func=ACT.Silu,
+                bias=conv_bias[:],
+                scale=1.0,
+            )
+        for half in range(2):
+            cols = slice(half * WIDTH // 2, (half + 1) * WIDTH // 2)
+            nc.sync.dma_start(out=out_1[:, cols], in_=conv[:, cols])
+
+        acc_right = project(1)
+        right = keep.tile([P, WIDTH], F32)
+        for nb in range(BANKS):
+            cols = slice(nb * BANK, (nb + 1) * BANK)
+            nc.vector.tensor_tensor(
+                out=right[:, cols], in0=acc_right[nb][:], in1=bias_bc[:, 1, cols], op=ALU.add
+            )
+            nc.sync.dma_start(out=out_2[:, cols], in_=right[:, cols])

@@ -17,13 +17,16 @@ K_PASS = P * PACK
 FEATURES = 2048
 PASSES = FEATURES // K_PASS
 WIDTH = 2048
+HALF = WIDTH // 2
 BANK = 512
 BANKS = WIDTH // BANK
 BLOCKS_PER_BANK = BANK // P
 TAPS = 4
 RUN = 4
 EPS = 1e-5
+CHUNKS = 2 * PASSES
 RAW_BUFS = 6
+V_COLS = (1024,) * (CHUNKS - 1) + (1280,)
 FLOPS = 2 * P * FEATURES * 2 * WIDTH
 
 
@@ -32,69 +35,109 @@ def tile_mlstmblock_pa_kernel(
 ):
     nc = tc.nc
     weights = (upL_w, upR_w)
+    outs = (out_0, out_2)
     with ExitStack() as ctx:
         keep = ctx.enter_context(tc.tile_pool(name="keep", bufs=1))
         raw_pool = ctx.enter_context(tc.tile_pool(name="raw", bufs=RAW_BUFS))
-        grouped_pool = ctx.enter_context(tc.tile_pool(name="grouped", bufs=2))
-        codes_pool = ctx.enter_context(tc.tile_pool(name="codes", bufs=3))
+        own_pool = ctx.enter_context(tc.tile_pool(name="own", bufs=2))
+        lent_pool = ctx.enter_context(tc.tile_pool(name="lent", bufs=3))
+        codes_pool = ctx.enter_context(tc.tile_pool(name="codes", bufs=6))
+        stage = ctx.enter_context(tc.tile_pool(name="stage", bufs=6))
         psum = ctx.enter_context(tc.psum_pool(name="psum", bufs=1))
+        ctx.enter_context(tc.manual_schedule())
 
-        raw = {}
+        bias_rows = keep.tile([P, 2, WIDTH], BF16)
+        nc.vector.memset(bias_rows[:], 0.0)
+        neg_half = keep.tile([P, 1], F32)
+        nc.gpsimd.memset(neg_half[:], -0.5)
+        ones = keep.tile([P, P], BF16)
+        nc.gpsimd.memset(ones[:], 1.0)
+        ident = keep.tile([P, P], F32)
+        make_identity(nc, ident[:])
 
-        def load_chunk(side, c):
-            raw[side, c] = raw_pool.tile([P, PACK, WIDTH], BF16, name="raw", tag="raw")
-            rows = weights[side][c * K_PASS : (c + 1) * K_PASS, :]
-            nc.sync.dma_start(out=raw[side, c][:], in_=rows.rearrange("(p j) n -> p j n", j=PACK))
-
-        chunks = [(side, c) for side in range(2) for c in range(PASSES)]
-
-        x_sb = keep.tile([P, FEATURES], BF16)
-        nc.sync.dma_start(out=x_sb[:], in_=x[:, :])
-
-        gain_bf = keep.tile([P, PASSES, PACK], BF16)
-        shift_bf = keep.tile([P, PASSES, PACK], BF16)
+        gain_bf = keep.tile([P, PASSES * PACK], BF16)
+        shift_bf = keep.tile([P, PASSES * PACK], BF16)
         taps_bf = keep.tile([P, TAPS], BF16)
         conv_b_bf = keep.tile([P, 1], BF16)
         with nc.allow_non_contiguous_dma(reason="two vectors of 2048 values, four to a piece"):
             nc.scalar.dma_start(
-                out=gain_bf[:], in_=ln_w.rearrange("(c p j) -> p c j", c=PASSES, j=PACK)
+                out=gain_bf[:].rearrange("p (c j) -> p c j", j=PACK),
+                in_=ln_w.rearrange("(c p j) -> p c j", c=PASSES, j=PACK),
             )
             nc.scalar.dma_start(
-                out=shift_bf[:], in_=ln_b.rearrange("(c p j) -> p c j", c=PASSES, j=PACK)
+                out=shift_bf[:].rearrange("p (c j) -> p c j", j=PACK),
+                in_=ln_b.rearrange("(c p j) -> p c j", c=PASSES, j=PACK),
             )
             nc.scalar.dma_start(out=taps_bf[:], in_=conv_w.partition_broadcast(P))
             nc.scalar.dma_start(out=conv_b_bf[:], in_=conv_b.partition_broadcast(P))
 
-        bias_bc = keep.tile([P, 2, WIDTH], BF16)
-        for side, c in chunks[:PASSES]:
-            load_chunk(side, c)
-        nc.sync.dma_start(out=bias_bc[:, 0, :], in_=upL_b.partition_broadcast(P))
-        nc.sync.dma_start(out=bias_bc[:, 1, :], in_=upR_b.partition_broadcast(P))
-        for side, c in chunks[PASSES:RAW_BUFS]:
-            load_chunk(side, c)
+        x_sb = keep.tile([P, FEATURES], BF16)
+        for h in range(2):
+            cols = slice(h * FEATURES // 2, (h + 1) * FEATURES // 2)
+            nc.sync.dma_start(out=x_sb[:, cols], in_=x[:, cols])
 
-        ident = keep.tile([P, P], F32)
-        make_identity(nc, ident[:])
-        eps = keep.tile([P, 1], F32)
-        nc.vector.memset(eps[:], EPS)
+        raw = {}
+
+        def load_chunk(i):
+            side, c = divmod(i, PASSES)
+            rows = weights[side][c * K_PASS : (c + 1) * K_PASS, :]
+            if i == 0:
+                raw[i] = raw_pool.tile([P, 2, PACK, HALF], BF16, name="raw", tag="raw")
+                for h in (1, 0):
+                    nc.sync.dma_start(
+                        out=raw[i][:, h],
+                        in_=rows[:, h * HALF : (h + 1) * HALF].rearrange("(p j) n -> p j n", j=PACK),
+                    )
+            else:
+                raw[i] = raw_pool.tile([P, PACK, WIDTH], BF16, name="raw", tag="raw")
+                nc.sync.dma_start(out=raw[i][:], in_=rows.rearrange("(p j) n -> p j n", j=PACK))
+
+        def raw_cols(i, lo, hi):
+            if i == 0:
+                h = lo // HALF
+                return raw[i][:, h, :, lo - h * HALF : hi - h * HALF]
+            return raw[i][:, :, lo:hi]
+
+        load_chunk(0)
+        warm = keep.tile([P, 1], F32)
+        nc.scalar.activation(out=warm[:], in_=neg_half[:], func=ACT.Silu)
+        nc.scalar.dma_start(out=bias_rows[0:1, 0, :], in_=upL_b.rearrange("(o n) -> o n", o=1))
+        nc.scalar.dma_start(out=bias_rows[0:1, 1, :], in_=upR_b.rearrange("(o n) -> o n", o=1))
+
+        for i in range(1, RAW_BUFS):
+            load_chunk(i)
 
         stats = keep.tile([P, PASSES, 6], F32)
         for c in range(PASSES):
             nc.vector.bn_stats(out=stats[:, c, :], in_=x_sb[:, c * K_PASS : (c + 1) * K_PASS])
         mean_var = keep.tile([P, 2], F32)
         nc.vector.bn_aggr(out=mean_var[:], in_=stats[:].rearrange("p c s -> p (c s)"))
-        std = keep.tile([P, 1], F32)
-        nc.scalar.activation(out=std[:], in_=mean_var[:, 1:2], func=ACT.Sqrt, bias=eps[:], scale=1.0)
+        var_eps = keep.tile([P, 1], F32)
+        nc.vector.tensor_scalar(
+            out=var_eps[:], in0=mean_var[:, 1:2], scalar1=EPS, scalar2=None, op0=ALU.add
+        )
         rstd = keep.tile([P, 1], F32)
-        nc.vector.reciprocal(out=rstd[:], in_=std[:])
+        nc.gpsimd.tensor_tensor(out=rstd[:], in0=var_eps[:], in1=neg_half[:], op=ALU.pow)
 
         gain = keep.tile([P, PASSES * PACK], F32)
-        shift = keep.tile([P, PASSES * PACK], F32)
-        nc.vector.tensor_copy(out=gain[:], in_=gain_bf[:].rearrange("p c j -> p (c j)"))
-        nc.vector.tensor_copy(out=shift[:], in_=shift_bf[:].rearrange("p c j -> p (c j)"))
+        nc.gpsimd.tensor_copy(out=gain[:], in_=gain_bf[:])
+        conv_bias = keep.tile([P, 1], F32)
+        nc.gpsimd.tensor_copy(out=conv_bias[:], in_=conv_b_bf[:])
+        band = keep.tile([P, 2 * P], F32)
+        nc.vector.memset(band[:], 0.0)
+        for d in range(TAPS):
+            nc.vector.scalar_tensor_tensor(
+                out=band[:, d : d + P],
+                in0=ident[:],
+                scalar=taps_bf[:, TAPS - 1 - d : TAPS - d],
+                in1=band[:, d : d + P],
+                op0=ALU.mult,
+                op1=ALU.add,
+            )
 
         z = keep.tile([P, PASSES, PACK, P], F32)
         x_by_word = x_sb[:].rearrange("b (c p j) -> b c j p", c=PASSES, j=PACK)
+        zT = []
         for c in range(PASSES):
             nc.vector.tensor_scalar(
                 out=z[:, c],
@@ -104,156 +147,248 @@ def tile_mlstmblock_pa_kernel(
                 op0=ALU.subtract,
                 op1=ALU.mult,
             )
+            zT.append(psum.tile([P, PACK, P], F32, name="zT", tag="bank%d" % (BANKS + c)))
+            for j in range(PACK):
+                nc.tensor.transpose(out=zT[c][:, j, :], in_=z[:, c, j, :], identity=ident[:])
 
         xn_rows = keep.tile([P, PASSES, PACK, P], BF16)
-        for c in range(PASSES):
-            zT = psum.tile([P, PACK, P], F32, name="zT", tag="bank%d" % (BANKS + c))
-            for j in range(PACK):
-                nc.tensor.transpose(out=zT[:, j, :], in_=z[:, c, j, :], identity=ident[:])
+
+        def norm_out(c):
             for j in range(PACK):
                 col = c * PACK + j
                 if c % 2 == 0:
                     nc.vector.tensor_scalar(
                         out=xn_rows[:, c, j, :],
-                        in0=zT[:, j, :],
-                        scalar1=gain[:, col : col + 1],
-                        scalar2=shift[:, col : col + 1],
+                        in0=zT[c][:, j, :],
+                        scalar1=gain_bf[:, col : col + 1],
+                        scalar2=shift_bf[:, col : col + 1],
                         op0=ALU.mult,
                         op1=ALU.add,
                     )
                 else:
                     nc.scalar.activation(
                         out=xn_rows[:, c, j, :],
-                        in_=zT[:, j, :],
+                        in_=zT[c][:, j, :],
                         func=ACT.Identity,
                         scale=gain[:, col : col + 1],
-                        bias=shift[:, col : col + 1],
+                        bias=shift_bf[:, col : col + 1],
                     )
 
         xn_grouped = keep.tile([P, PASSES, P, PACK], BF16, align_bytes=64)
-        nc.vector.tensor_copy(out=xn_grouped[:], in_=xn_rows[:].rearrange("p c j b -> p c b j"))
         xn_codes = keep.tile([P, PASSES * P], U32, align_bytes=64)
         xn_scales = keep.tile([P, PASSES * P], U8, align_bytes=64)
-        nc.vector.quantize_mx(
-            out=xn_codes[:].bitcast(FP8X4),
-            scales=xn_scales[:],
-            in_=xn_grouped[:].rearrange("p c b j -> p (c b j)"),
-        )
 
-        taps = keep.tile([P, TAPS], F32)
-        nc.vector.tensor_copy(out=taps[:], in_=taps_bf[:])
-        conv_bias = keep.tile([P, 1], F32)
-        nc.vector.tensor_copy(out=conv_bias[:], in_=conv_b_bf[:])
-        band = keep.tile([P, 2 * P], F32)
-        nc.vector.memset(band[:], 0.0)
-        for d in range(TAPS):
-            nc.vector.scalar_tensor_tensor(
-                out=band[:, d : d + P],
-                in0=ident[:],
-                scalar=taps[:, TAPS - 1 - d : TAPS - d],
-                in1=band[:, d : d + P],
-                op0=ALU.mult,
-                op1=ALU.add,
-            )
+        bias_bc = keep.tile([P, 2, WIDTH], BF16)
 
-        def project(side):
-            acc = [
-                psum.tile([P, BANK], F32, name="acc", tag="bank%d" % (side * BANKS + nb))
-                for nb in range(BANKS)
-            ]
-            for c in range(PASSES):
-                grouped = []
-                for nb in range(BANKS):
-                    piece = grouped_pool.tile(
-                        [P, BANK, PACK], BF16, align_bytes=64, name="grouped", tag="grouped%d" % nb
-                    )
-                    copy = nc.vector.tensor_copy if nb < BANKS // 2 else nc.scalar.copy
-                    copy(
-                        out=piece[:].rearrange("p (q i) j -> p q j i", i=RUN),
-                        in_=raw[side, c][:, :, nb * BANK : (nb + 1) * BANK].rearrange(
-                            "p j (q i) -> p q j i", i=RUN
-                        ),
-                    )
-                    grouped.append(piece)
-                done = chunks.index((side, c))
-                if done + RAW_BUFS < len(chunks):
-                    load_chunk(*chunks[done + RAW_BUFS])
-                for nb in range(BANKS):
-                    codes = codes_pool.tile([P, BANK], U32, align_bytes=64, name="codes", tag="codes%d" % nb)
-                    scales = codes_pool.tile([P, BANK], U8, align_bytes=64, name="scales", tag="scales%d" % nb)
-                    nc.vector.quantize_mx(
-                        out=codes[:].bitcast(FP8X4),
-                        scales=scales[:],
-                        in_=grouped[nb][:].rearrange("p n j -> p (n j)"),
-                    )
-                    nc.tensor.matmul_mx(
-                        out=acc[nb][:],
-                        lhsT=xn_codes[:, c * P : (c + 1) * P].bitcast(FP8X4),
-                        lhsT_scale=xn_scales[:, c * P : (c + 1) * P],
-                        rhs=codes[:].bitcast(FP8X4),
-                        rhs_scale=scales[:],
-                        start=(c == 0),
-                        stop=(c == PASSES - 1),
-                    )
-            return acc
-
-        acc_left = project(0)
-        left = keep.tile([P, WIDTH], F32)
-        for nb in range(BANKS):
-            cols = slice(nb * BANK, (nb + 1) * BANK)
-            nc.vector.tensor_tensor(
-                out=left[:, cols], in0=acc_left[nb][:], in1=bias_bc[:, 0, cols], op=ALU.add
-            )
-        for half in range(2):
-            cols = slice(half * WIDTH // 2, (half + 1) * WIDTH // 2)
-            nc.sync.dma_start(out=out_0[:, cols], in_=left[:, cols])
-
-        leftT = keep.tile([P, BANKS * BLOCKS_PER_BANK, P], F32)
-        conv = keep.tile([P, WIDTH], F32)
-        for nb in range(BANKS):
-            first = nb * BLOCKS_PER_BANK
-            leftT_ps = psum.tile([P, BLOCKS_PER_BANK, P], F32, name="leftT_ps", tag="bank%d" % (nb % 2))
-            for q in range(BLOCKS_PER_BANK):
-                nc.tensor.transpose(
-                    out=leftT_ps[:, q, :],
-                    in_=left[:, (first + q) * P : (first + q + 1) * P],
-                    identity=ident[:],
-                )
-            nc.scalar.copy(out=leftT[:, first : first + BLOCKS_PER_BANK, :], in_=leftT_ps[:])
-            conv_ps = psum.tile([P, BANK], F32, name="conv_ps", tag="bank%d" % (2 + nb % 2))
-            for q in range(BLOCKS_PER_BANK):
-                block = first + q
-                nc.tensor.matmul(
-                    out=conv_ps[:, q * P : (q + 1) * P],
-                    lhsT=leftT[:, block, :],
-                    rhs=band[:, 0:P],
-                    start=True,
-                    stop=(block == 0),
-                )
-                if block > 0:
+        def spread_biases():
+            for half in range(4):
+                side, part = divmod(half, 2)
+                spread = psum.tile([P, HALF], BF16, name="spread", tag="bank%d" % half)
+                for u in range(2):
+                    first = part * HALF + u * BANK
                     nc.tensor.matmul(
-                        out=conv_ps[:, q * P : (q + 1) * P],
-                        lhsT=leftT[:, block - 1, :],
-                        rhs=band[:, P : 2 * P],
-                        start=False,
+                        out=spread[:, u * BANK : (u + 1) * BANK],
+                        lhsT=ones[:],
+                        rhs=bias_rows[:, side, first : first + BANK],
+                        start=True,
                         stop=True,
                     )
-            nc.scalar.activation(
-                out=conv[:, nb * BANK : (nb + 1) * BANK],
-                in_=conv_ps[:],
-                func=ACT.Silu,
-                bias=conv_bias[:],
-                scale=1.0,
-            )
-        for half in range(2):
-            cols = slice(half * WIDTH // 2, (half + 1) * WIDTH // 2)
-            nc.sync.dma_start(out=out_1[:, cols], in_=conv[:, cols])
+                nc.scalar.copy(out=bias_bc[:, side, part * HALF : (part + 1) * HALF], in_=spread[:])
 
-        acc_right = project(1)
-        right = keep.tile([P, WIDTH], F32)
-        for nb in range(BANKS):
-            cols = slice(nb * BANK, (nb + 1) * BANK)
-            nc.vector.tensor_tensor(
-                out=right[:, cols], in0=acc_right[nb][:], in1=bias_bc[:, 1, cols], op=ALU.add
+        grouped = {}
+        acc = {}
+        waiting = []
+
+        def regroup(engine_copy, i, lo, hi):
+            h = lo // HALF
+            engine_copy(
+                out=grouped[i, h][:, lo - h * HALF : hi - h * HALF, :].rearrange(
+                    "p (q i) j -> p q j i", i=RUN
+                ),
+                in_=raw_cols(i, lo, hi).rearrange("p j (q i) -> p q j i", i=RUN),
             )
-            nc.sync.dma_start(out=out_2[:, cols], in_=right[:, cols])
+
+        def quantise(i, h, pieces=1):
+            codes = codes_pool.tile([P, HALF], U32, align_bytes=64, name="codes", tag="codes")
+            scales = codes_pool.tile([P, HALF], U8, align_bytes=64, name="scales", tag="scales")
+            wide = HALF // pieces
+            for u in range(pieces):
+                nc.vector.quantize_mx(
+                    out=codes[:, u * wide : (u + 1) * wide].bitcast(FP8X4),
+                    scales=scales[:, u * wide : (u + 1) * wide],
+                    in_=grouped[i, h][:, u * wide : (u + 1) * wide, :].rearrange("p n j -> p (n j)"),
+                )
+                if pieces > 1:
+                    add_bias(1, u)
+            for u in range(HALF // BANK):
+                waiting.append((i, h * (HALF // BANK) + u, codes, scales, u * BANK))
+
+        def multiply():
+            for i, nb, codes, scales, first in waiting:
+                side, c = divmod(i, PASSES)
+                if c == 0:
+                    acc[side, nb] = psum.tile(
+                        [P, BANK], F32, name="acc", tag="bank%d" % (side * BANKS + nb)
+                    )
+                nc.tensor.matmul_mx(
+                    out=acc[side, nb][:],
+                    lhsT=xn_codes[:, c * P : (c + 1) * P].bitcast(FP8X4),
+                    lhsT_scale=xn_scales[:, c * P : (c + 1) * P],
+                    rhs=codes[:, first : first + BANK].bitcast(FP8X4),
+                    rhs_scale=scales[:, first : first + BANK],
+                    start=(c == 0),
+                    stop=(c == PASSES - 1),
+                )
+            waiting.clear()
+
+        biased = {}
+
+        def add_bias(side, nb):
+            cols = slice(nb * BANK, (nb + 1) * BANK)
+            biased[side, nb] = stage.tile([P, BANK], F32, name="staged", tag="staged")
+            nc.vector.tensor_tensor(
+                out=biased[side, nb][:], in0=acc[side, nb][:], in1=bias_bc[:, side, cols], op=ALU.add
+            )
+            nc.sync.dma_start(out=outs[side][:, cols], in_=biased[side, nb][:])
+
+        leftT = keep.tile([P, BANKS * BLOCKS_PER_BANK, P], F32)
+        leftT_ps = {}
+        conv_ps = {}
+
+        def turn_left(nb):
+            leftT_ps[nb] = psum.tile(
+                [P, BLOCKS_PER_BANK, P], F32, name="leftT_ps", tag="bank%d" % (nb % 2)
+            )
+            for q in range(BLOCKS_PER_BANK):
+                nc.tensor.transpose(
+                    out=leftT_ps[nb][:, q, :],
+                    in_=biased[0, nb][:, q * P : (q + 1) * P],
+                    identity=ident[:],
+                )
+
+        def keep_leftT(nb):
+            first = nb * BLOCKS_PER_BANK
+            nc.scalar.copy(out=leftT[:, first : first + BLOCKS_PER_BANK, :], in_=leftT_ps[nb][:])
+
+        def convolve(nb):
+            conv_ps[nb] = psum.tile([P, BANK], F32, name="conv_ps", tag="bank%d" % (2 + nb % 2))
+            for q in range(BLOCKS_PER_BANK):
+                block = nb * BLOCKS_PER_BANK + q
+                if block == 0:
+                    nc.tensor.matmul(
+                        out=conv_ps[nb][:, 0:P], lhsT=leftT[:, 0, :], rhs=band[:, 0:P], start=True, stop=True
+                    )
+                    continue
+                nc.tensor.matmul(
+                    out=conv_ps[nb][:, q * P : q * P + TAPS],
+                    lhsT=leftT[:, block - 1, :],
+                    rhs=band[:, P : P + TAPS],
+                    start=True,
+                    stop=False,
+                )
+                nc.tensor.matmul(
+                    out=conv_ps[nb][:, q * P : q * P + TAPS],
+                    lhsT=leftT[:, block, :],
+                    rhs=band[:, 0:TAPS],
+                    start=False,
+                    stop=True,
+                )
+                nc.tensor.matmul(
+                    out=conv_ps[nb][:, q * P + TAPS : (q + 1) * P],
+                    lhsT=leftT[:, block, :],
+                    rhs=band[:, TAPS:P],
+                    start=True,
+                    stop=True,
+                )
+
+        def silu_out(nb):
+            cols = slice(nb * BANK, (nb + 1) * BANK)
+            conv = stage.tile([P, BANK], F32, name="staged", tag="staged")
+            nc.scalar.activation(
+                out=conv[:], in_=conv_ps[nb][:], func=ACT.Silu, bias=conv_bias[:], scale=1.0
+            )
+            nc.sync.dma_start(out=out_1[:, cols], in_=conv[:])
+
+        lagging = []
+        for i in range(CHUNKS + 1):
+            late = lagging
+            lagging = []
+            own = []
+            vector_copies = []
+            if i < CHUNKS:
+                cut = V_COLS[i]
+                scalar_copies = []
+                for h in range(2):
+                    lo, hi = h * HALF, (h + 1) * HALF
+                    pool = own_pool if hi <= cut else lent_pool
+                    grouped[i, h] = pool.tile(
+                        [P, HALF, PACK], BF16, align_bytes=64, name="grouped", tag="grouped"
+                    )
+                    if hi <= cut:
+                        own.append(h)
+                    else:
+                        lagging.append(h)
+                    for nb in (2 * h, 2 * h + 1):
+                        lo, hi = nb * BANK, (nb + 1) * BANK
+                        if lo < cut:
+                            vector_copies.append((lo, min(hi, cut)))
+                        if hi > cut:
+                            scalar_copies.append((max(lo, cut), hi))
+                for step, (lo, hi) in enumerate(scalar_copies):
+                    regroup(nc.scalar.copy, i, lo, hi)
+                    if (i, step) == (PASSES + 1, 0):
+                        keep_leftT(0)
+                        convolve(0)
+                        turn_left(2)
+                        keep_leftT(1)
+                        convolve(1)
+                        turn_left(3)
+                    if (i, step) == (PASSES + 1, 1):
+                        silu_out(0)
+                        keep_leftT(2)
+                        convolve(2)
+                    if (i, step) == (PASSES + 2, 0):
+                        silu_out(1)
+                        keep_leftT(3)
+                        convolve(3)
+                    if (i, step) == (PASSES + 2, 1):
+                        silu_out(2)
+                    if (i, step) == (PASSES + 3, 0):
+                        silu_out(3)
+                    if i == 0 and step == 0:
+                        norm_out(1)
+                        norm_out(3)
+                        spread_biases()
+
+            for step, (lo, hi) in enumerate(vector_copies):
+                regroup(nc.vector.tensor_copy, i, lo, hi)
+                if i == 0 and step == 0:
+                    norm_out(0)
+                    norm_out(2)
+                if i == PASSES:
+                    add_bias(0, step)
+                    turn_left(step)
+            if i < CHUNKS and i + RAW_BUFS < CHUNKS:
+                load_chunk(i + RAW_BUFS)
+            if i == 0:
+                nc.vector.tensor_copy(
+                    out=xn_grouped[:], in_=xn_rows[:].rearrange("p c j b -> p c b j")
+                )
+            for h in late:
+                quantise(i - 1, h, pieces=(HALF // BANK if i == CHUNKS else 1))
+                multiply()
+            for h in own:
+                quantise(i, h)
+                if i == 0:
+                    nc.vector.quantize_mx(
+                        out=xn_codes[:].bitcast(FP8X4),
+                        scales=xn_scales[:],
+                        in_=xn_grouped[:].rearrange("p c b j -> p (c b j)"),
+                    )
+                multiply()
+            if i == PASSES:
+                add_bias(0, 2)
+                add_bias(0, 3)
+            if i == CHUNKS:
+                add_bias(1, 2)
+                add_bias(1, 3)

@@ -22,6 +22,10 @@ BANK = 512
 BANKS = WIDTH // BANK
 BLOCKS_PER_BANK = BANK // P
 TAPS = 4
+STEP = P - (TAPS - 1)
+WINDOWS = -(-WIDTH // STEP)
+WINDOWS_PER_BANK = BANK // P
+PAD = 8
 RUN = 4
 EPS = 1e-5
 CHUNKS = 2 * PASSES
@@ -39,14 +43,13 @@ def tile_mlstmblock_pa_kernel(
     with ExitStack() as ctx:
         keep = ctx.enter_context(tc.tile_pool(name="keep", bufs=1))
         raw_pool = ctx.enter_context(tc.tile_pool(name="raw", bufs=RAW_BUFS))
-        own_pool = ctx.enter_context(tc.tile_pool(name="own", bufs=2))
-        lent_pool = ctx.enter_context(tc.tile_pool(name="lent", bufs=3))
+        grouped_pool = ctx.enter_context(tc.tile_pool(name="grouped", bufs=6))
         codes_pool = ctx.enter_context(tc.tile_pool(name="codes", bufs=6))
-        stage = ctx.enter_context(tc.tile_pool(name="stage", bufs=6))
+        stage = ctx.enter_context(tc.tile_pool(name="stage", bufs=4))
         psum = ctx.enter_context(tc.psum_pool(name="psum", bufs=1))
         ctx.enter_context(tc.manual_schedule())
 
-        bias_rows = keep.tile([P, 2, WIDTH], BF16)
+        bias_rows = keep.tile([P, 2, WIDTH], BF16, name="bias_rows", tag="early0")
         nc.vector.memset(bias_rows[:], 0.0)
         neg_half = keep.tile([P, 1], F32)
         nc.gpsimd.memset(neg_half[:], -0.5)
@@ -55,22 +58,6 @@ def tile_mlstmblock_pa_kernel(
         ident = keep.tile([P, P], F32)
         make_identity(nc, ident[:])
 
-        gain_bf = keep.tile([P, PASSES * PACK], BF16)
-        shift_bf = keep.tile([P, PASSES * PACK], BF16)
-        taps_bf = keep.tile([P, TAPS], BF16)
-        conv_b_bf = keep.tile([P, 1], BF16)
-        with nc.allow_non_contiguous_dma(reason="two vectors of 2048 values, four to a piece"):
-            nc.scalar.dma_start(
-                out=gain_bf[:].rearrange("p (c j) -> p c j", j=PACK),
-                in_=ln_w.rearrange("(c p j) -> p c j", c=PASSES, j=PACK),
-            )
-            nc.scalar.dma_start(
-                out=shift_bf[:].rearrange("p (c j) -> p c j", j=PACK),
-                in_=ln_b.rearrange("(c p j) -> p c j", c=PASSES, j=PACK),
-            )
-            nc.scalar.dma_start(out=taps_bf[:], in_=conv_w.partition_broadcast(P))
-            nc.scalar.dma_start(out=conv_b_bf[:], in_=conv_b.partition_broadcast(P))
-
         x_sb = keep.tile([P, FEATURES], BF16)
         for h in range(2):
             cols = slice(h * FEATURES // 2, (h + 1) * FEATURES // 2)
@@ -78,19 +65,14 @@ def tile_mlstmblock_pa_kernel(
 
         raw = {}
 
-        def load_chunk(i):
+        def load_rows(i, out, lo, hi):
             side, c = divmod(i, PASSES)
-            rows = weights[side][c * K_PASS : (c + 1) * K_PASS, :]
-            if i == 0:
-                raw[i] = raw_pool.tile([P, 2, PACK, HALF], BF16, name="raw", tag="raw")
-                for h in (1, 0):
-                    nc.sync.dma_start(
-                        out=raw[i][:, h],
-                        in_=rows[:, h * HALF : (h + 1) * HALF].rearrange("(p j) n -> p j n", j=PACK),
-                    )
-            else:
-                raw[i] = raw_pool.tile([P, PACK, WIDTH], BF16, name="raw", tag="raw")
-                nc.sync.dma_start(out=raw[i][:], in_=rows.rearrange("(p j) n -> p j n", j=PACK))
+            rows = weights[side][c * K_PASS : (c + 1) * K_PASS, lo:hi]
+            nc.sync.dma_start(out=out, in_=rows.rearrange("(p j) n -> p j n", j=PACK))
+
+        def load_chunk(i):
+            raw[i] = raw_pool.tile([P, PACK, WIDTH], BF16, name="raw", tag="raw")
+            load_rows(i, raw[i][:], 0, WIDTH)
 
         def raw_cols(i, lo, hi):
             if i == 0:
@@ -98,14 +80,31 @@ def tile_mlstmblock_pa_kernel(
                 return raw[i][:, h, :, lo - h * HALF : hi - h * HALF]
             return raw[i][:, :, lo:hi]
 
-        load_chunk(0)
-        warm = keep.tile([P, 1], F32)
-        nc.scalar.activation(out=warm[:], in_=neg_half[:], func=ACT.Silu)
-        nc.scalar.dma_start(out=bias_rows[0:1, 0, :], in_=upL_b.rearrange("(o n) -> o n", o=1))
-        nc.scalar.dma_start(out=bias_rows[0:1, 1, :], in_=upR_b.rearrange("(o n) -> o n", o=1))
-
+        raw[0] = raw_pool.tile([P, 2, PACK, HALF], BF16, name="raw", tag="raw")
+        load_rows(0, raw[0][:, 1], HALF, WIDTH)
+        gain_bf = keep.tile([P, PASSES * PACK], BF16)
+        shift_bf = keep.tile([P, PASSES * PACK], BF16)
+        taps_bf = keep.tile([P, TAPS], BF16)
+        conv_b_bf = keep.tile([P, 1], BF16)
+        with nc.allow_non_contiguous_dma(reason="two vectors of 2048 values, four to a piece"):
+            nc.sync.dma_start(
+                out=gain_bf[:].rearrange("p (c j) -> p c j", j=PACK),
+                in_=ln_w.rearrange("(c p j) -> p c j", c=PASSES, j=PACK),
+            )
+            nc.sync.dma_start(
+                out=shift_bf[:].rearrange("p (c j) -> p c j", j=PACK),
+                in_=ln_b.rearrange("(c p j) -> p c j", c=PASSES, j=PACK),
+            )
+            nc.sync.dma_start(out=taps_bf[:], in_=conv_w.partition_broadcast(P))
+            nc.sync.dma_start(out=conv_b_bf[:], in_=conv_b.partition_broadcast(P))
+        load_rows(0, raw[0][:, 0], 0, HALF)
+        nc.sync.dma_start(out=bias_rows[0:1, 0, :], in_=upL_b.rearrange("(o n) -> o n", o=1))
+        nc.sync.dma_start(out=bias_rows[0:1, 1, :], in_=upR_b.rearrange("(o n) -> o n", o=1))
         for i in range(1, RAW_BUFS):
             load_chunk(i)
+
+        warm = keep.tile([P, 1], F32)
+        nc.scalar.activation(out=warm[:], in_=neg_half[:], func=ACT.Silu)
 
         stats = keep.tile([P, PASSES, 6], F32)
         for c in range(PASSES):
@@ -123,19 +122,21 @@ def tile_mlstmblock_pa_kernel(
         nc.gpsimd.tensor_copy(out=gain[:], in_=gain_bf[:])
         conv_bias = keep.tile([P, 1], F32)
         nc.gpsimd.tensor_copy(out=conv_bias[:], in_=conv_b_bf[:])
-        band = keep.tile([P, 2 * P], F32)
-        nc.vector.memset(band[:], 0.0)
-        for d in range(TAPS):
+        band = keep.tile([P, STEP], F32)
+        nc.vector.tensor_scalar(
+            out=band[:], in0=ident[:, 0:STEP], scalar1=taps_bf[:, 0:1], scalar2=None, op0=ALU.mult
+        )
+        for t in range(1, TAPS):
             nc.vector.scalar_tensor_tensor(
-                out=band[:, d : d + P],
-                in0=ident[:],
-                scalar=taps_bf[:, TAPS - 1 - d : TAPS - d],
-                in1=band[:, d : d + P],
+                out=band[:],
+                in0=ident[:, t : t + STEP],
+                scalar=taps_bf[:, t : t + 1],
+                in1=band[:],
                 op0=ALU.mult,
                 op1=ALU.add,
             )
 
-        z = keep.tile([P, PASSES, PACK, P], F32)
+        z = keep.tile([P, PASSES, PACK, P], F32, name="z", tag="early1")
         x_by_word = x_sb[:].rearrange("b (c p j) -> b c j p", c=PASSES, j=PACK)
         zT = []
         for c in range(PASSES):
@@ -180,20 +181,28 @@ def tile_mlstmblock_pa_kernel(
 
         bias_bc = keep.tile([P, 2, WIDTH], BF16)
 
+        spread = {}
+
         def spread_biases():
             for half in range(4):
                 side, part = divmod(half, 2)
-                spread = psum.tile([P, HALF], BF16, name="spread", tag="bank%d" % half)
+                spread[half] = psum.tile([P, HALF], BF16, name="spread", tag="bank%d" % (BANKS + half))
                 for u in range(2):
                     first = part * HALF + u * BANK
                     nc.tensor.matmul(
-                        out=spread[:, u * BANK : (u + 1) * BANK],
+                        out=spread[half][:, u * BANK : (u + 1) * BANK],
                         lhsT=ones[:],
                         rhs=bias_rows[:, side, first : first + BANK],
                         start=True,
                         stop=True,
                     )
-                nc.scalar.copy(out=bias_bc[:, side, part * HALF : (part + 1) * HALF], in_=spread[:])
+
+        def keep_biases():
+            for half in range(4):
+                side, part = divmod(half, 2)
+                nc.scalar.copy(
+                    out=bias_bc[:, side, part * HALF : (part + 1) * HALF], in_=spread[half][:]
+                )
 
         grouped = {}
         acc = {}
@@ -241,73 +250,67 @@ def tile_mlstmblock_pa_kernel(
                 )
             waiting.clear()
 
-        biased = {}
+        left = None
+        conv = None
 
         def add_bias(side, nb):
             cols = slice(nb * BANK, (nb + 1) * BANK)
-            biased[side, nb] = stage.tile([P, BANK], F32, name="staged", tag="staged")
+            if side == 0:
+                biased = left[:, PAD + nb * BANK : PAD + (nb + 1) * BANK]
+            else:
+                staged = stage.tile([P, BANK], F32, name="staged", tag="staged")
+                biased = staged[:]
             nc.vector.tensor_tensor(
-                out=biased[side, nb][:], in0=acc[side, nb][:], in1=bias_bc[:, side, cols], op=ALU.add
+                out=biased, in0=acc[side, nb][:], in1=bias_bc[:, side, cols], op=ALU.add
             )
-            nc.sync.dma_start(out=outs[side][:, cols], in_=biased[side, nb][:])
+            nc.sync.dma_start(out=outs[side][:, cols], in_=biased)
 
-        leftT = keep.tile([P, BANKS * BLOCKS_PER_BANK, P], F32)
+        leftT = keep.tile([P, WINDOWS, P], F32)
         leftT_ps = {}
         conv_ps = {}
 
-        def turn_left(nb):
-            leftT_ps[nb] = psum.tile(
-                [P, BLOCKS_PER_BANK, P], F32, name="leftT_ps", tag="bank%d" % (nb % 2)
+        def windows_of(g):
+            return range(g * WINDOWS_PER_BANK, min((g + 1) * WINDOWS_PER_BANK, WINDOWS))
+
+        def turn_left(g):
+            leftT_ps[g] = psum.tile(
+                [P, WINDOWS_PER_BANK, P], F32, name="leftT_ps", tag="bank%d" % (g % 2)
             )
-            for q in range(BLOCKS_PER_BANK):
+            for q, w in enumerate(windows_of(g)):
+                first = min(w * STEP, WIDTH - STEP) + PAD - (TAPS - 1)
                 nc.tensor.transpose(
-                    out=leftT_ps[nb][:, q, :],
-                    in_=biased[0, nb][:, q * P : (q + 1) * P],
-                    identity=ident[:],
+                    out=leftT_ps[g][:, q, :], in_=left[:, first : first + P], identity=ident[:]
                 )
 
-        def keep_leftT(nb):
-            first = nb * BLOCKS_PER_BANK
-            nc.scalar.copy(out=leftT[:, first : first + BLOCKS_PER_BANK, :], in_=leftT_ps[nb][:])
+        def keep_leftT(g):
+            ws = windows_of(g)
+            nc.scalar.copy(out=leftT[:, ws.start : ws.stop, :], in_=leftT_ps[g][:, 0 : len(ws), :])
 
-        def convolve(nb):
-            conv_ps[nb] = psum.tile([P, BANK], F32, name="conv_ps", tag="bank%d" % (2 + nb % 2))
-            for q in range(BLOCKS_PER_BANK):
-                block = nb * BLOCKS_PER_BANK + q
-                if block == 0:
-                    nc.tensor.matmul(
-                        out=conv_ps[nb][:, 0:P], lhsT=leftT[:, 0, :], rhs=band[:, 0:P], start=True, stop=True
-                    )
-                    continue
+        def convolve(g):
+            conv_ps[g] = psum.tile([P, BANK], F32, name="conv_ps", tag="bank%d" % (2 + g % 2))
+            for q, w in enumerate(windows_of(g)):
+                skip = w * STEP - min(w * STEP, WIDTH - STEP)
                 nc.tensor.matmul(
-                    out=conv_ps[nb][:, q * P : q * P + TAPS],
-                    lhsT=leftT[:, block - 1, :],
-                    rhs=band[:, P : P + TAPS],
-                    start=True,
-                    stop=False,
-                )
-                nc.tensor.matmul(
-                    out=conv_ps[nb][:, q * P : q * P + TAPS],
-                    lhsT=leftT[:, block, :],
-                    rhs=band[:, 0:TAPS],
-                    start=False,
-                    stop=True,
-                )
-                nc.tensor.matmul(
-                    out=conv_ps[nb][:, q * P + TAPS : (q + 1) * P],
-                    lhsT=leftT[:, block, :],
-                    rhs=band[:, TAPS:P],
+                    out=conv_ps[g][:, q * STEP : (q + 1) * STEP - skip],
+                    lhsT=leftT[:, w, :],
+                    rhs=band[:, skip:STEP],
                     start=True,
                     stop=True,
                 )
 
-        def silu_out(nb):
-            cols = slice(nb * BANK, (nb + 1) * BANK)
-            conv = stage.tile([P, BANK], F32, name="staged", tag="staged")
+        def silu_out(g):
+            first = g * WINDOWS_PER_BANK * STEP
+            last = min(first + WINDOWS_PER_BANK * STEP, WIDTH)
             nc.scalar.activation(
-                out=conv[:], in_=conv_ps[nb][:], func=ACT.Silu, bias=conv_bias[:], scale=1.0
+                out=conv[:, first:last],
+                in_=conv_ps[g][:, 0 : last - first],
+                func=ACT.Silu,
+                bias=conv_bias[:],
+                scale=1.0,
             )
-            nc.sync.dma_start(out=out_1[:, cols], in_=conv[:])
+            if g > 0:
+                cols = slice((g - 1) * BANK, g * BANK)
+                nc.scalar.dma_start(out=out_1[:, cols], in_=conv[:, cols])
 
         lagging = []
         for i in range(CHUNKS + 1):
@@ -320,8 +323,7 @@ def tile_mlstmblock_pa_kernel(
                 scalar_copies = []
                 for h in range(2):
                     lo, hi = h * HALF, (h + 1) * HALF
-                    pool = own_pool if hi <= cut else lent_pool
-                    grouped[i, h] = pool.tile(
+                    grouped[i, h] = grouped_pool.tile(
                         [P, HALF, PACK], BF16, align_bytes=64, name="grouped", tag="grouped"
                     )
                     if hi <= cut:
@@ -336,29 +338,30 @@ def tile_mlstmblock_pa_kernel(
                             scalar_copies.append((max(lo, cut), hi))
                 for step, (lo, hi) in enumerate(scalar_copies):
                     regroup(nc.scalar.copy, i, lo, hi)
-                    if (i, step) == (PASSES + 1, 0):
-                        keep_leftT(0)
-                        convolve(0)
-                        turn_left(2)
-                        keep_leftT(1)
-                        convolve(1)
-                        turn_left(3)
-                    if (i, step) == (PASSES + 1, 1):
-                        silu_out(0)
-                        keep_leftT(2)
-                        convolve(2)
-                    if (i, step) == (PASSES + 2, 0):
-                        silu_out(1)
-                        keep_leftT(3)
-                        convolve(3)
-                    if (i, step) == (PASSES + 2, 1):
-                        silu_out(2)
-                    if (i, step) == (PASSES + 3, 0):
-                        silu_out(3)
-                    if i == 0 and step == 0:
+                    if (i, step) == (0, 1):
                         norm_out(1)
                         norm_out(3)
-                        spread_biases()
+                    if (i, step) == (PASSES - 1, 0):
+                        keep_biases()
+                    if (i, step) == (PASSES + 1, 1):
+                        keep_leftT(0)
+                        keep_leftT(1)
+                    if (i, step) == (PASSES + 2, 1):
+                        keep_leftT(2)
+                        keep_leftT(3)
+                        silu_out(0)
+                        silu_out(1)
+                    if (i, step) == (PASSES + 3, 1):
+                        keep_leftT(4)
+                        silu_out(2)
+                        silu_out(3)
+            if i == CHUNKS:
+                silu_out(4)
+
+            if i == PASSES - 1:
+                left = keep.tile([P, PAD + WIDTH], F32, name="left", tag="early0")
+                nc.gpsimd.memset(left[:, 0:PAD], 0.0)
+                conv = keep.tile([P, WIDTH], F32, name="conv", tag="early1")
 
             for step, (lo, hi) in enumerate(vector_copies):
                 regroup(nc.vector.tensor_copy, i, lo, hi)
@@ -367,7 +370,6 @@ def tile_mlstmblock_pa_kernel(
                     norm_out(2)
                 if i == PASSES:
                     add_bias(0, step)
-                    turn_left(step)
             if i < CHUNKS and i + RAW_BUFS < CHUNKS:
                 load_chunk(i + RAW_BUFS)
             if i == 0:
@@ -386,9 +388,24 @@ def tile_mlstmblock_pa_kernel(
                         in_=xn_grouped[:].rearrange("p c b j -> p (c b j)"),
                     )
                 multiply()
+            if i == 1:
+                spread_biases()
             if i == PASSES:
                 add_bias(0, 2)
                 add_bias(0, 3)
+                turn_left(0)
+                turn_left(1)
+            if i == PASSES + 1:
+                turn_left(2)
+                turn_left(3)
+                convolve(0)
+                convolve(1)
+            if i == PASSES + 2:
+                turn_left(4)
+                convolve(2)
+                convolve(3)
+            if i == PASSES + 3:
+                convolve(4)
             if i == CHUNKS:
                 add_bias(1, 2)
                 add_bias(1, 3)

@@ -26,7 +26,7 @@ STEP = P - (TAPS - 1)
 WINDOWS = -(-WIDTH // STEP)
 WINDOWS_PER_BANK = BANK // P
 PAD = 8
-RUN = 4
+RUN = 8
 EPS = 1e-5
 CHUNKS = 2 * PASSES
 RAW_BUFS = 6

@@ -50,13 +50,13 @@ def tile_mlstmblock_pa_kernel(
         ctx.enter_context(tc.manual_schedule())
 
         bias_rows = keep.tile([P, 2, WIDTH], BF16, name="bias_rows", tag="early0")
-        nc.vector.memset(bias_rows[:], 0.0)
         neg_half = keep.tile([P, 1], F32)
         nc.gpsimd.memset(neg_half[:], -0.5)
-        ones = keep.tile([P, P], BF16)
-        nc.gpsimd.memset(ones[:], 1.0)
         ident = keep.tile([P, P], F32)
         make_identity(nc, ident[:])
+        nc.gpsimd.memset(bias_rows[:].rearrange("p s n -> p (s n)").bitcast(F32), 0.0)
+        ones = keep.tile([P, P], BF16)
+        nc.gpsimd.memset(ones[:], 1.0)
 
         x_sb = keep.tile([P, FEATURES], BF16)
         for h in range(2):

@@ -49,14 +49,10 @@ def tile_mlstmblock_pa_kernel(
         psum = ctx.enter_context(tc.psum_pool(name="psum", bufs=1))
         ctx.enter_context(tc.manual_schedule())
 
-        bias_rows = keep.tile([P, 2, WIDTH], BF16, name="bias_rows", tag="early0")
         neg_half = keep.tile([P, 1], F32)
         nc.gpsimd.memset(neg_half[:], -0.5)
         ident = keep.tile([P, P], F32)
         make_identity(nc, ident[:])
-        nc.gpsimd.memset(bias_rows[:].rearrange("p s n -> p (s n)").bitcast(F32), 0.0)
-        ones = keep.tile([P, P], BF16)
-        nc.gpsimd.memset(ones[:], 1.0)
 
         x_sb = keep.tile([P, FEATURES], BF16)
         for h in range(2):
@@ -98,10 +94,11 @@ def tile_mlstmblock_pa_kernel(
             nc.sync.dma_start(out=taps_bf[:], in_=conv_w.partition_broadcast(P))
             nc.sync.dma_start(out=conv_b_bf[:], in_=conv_b.partition_broadcast(P))
         load_rows(0, raw[0][:, 0], 0, HALF)
-        nc.sync.dma_start(out=bias_rows[0:1, 0, :], in_=upL_b.rearrange("(o n) -> o n", o=1))
-        nc.sync.dma_start(out=bias_rows[0:1, 1, :], in_=upR_b.rearrange("(o n) -> o n", o=1))
+        bias_bc = keep.tile([P, 2, WIDTH], BF16)
         for i in range(1, RAW_BUFS):
             load_chunk(i)
+            if i == PASSES - 1:
+                nc.sync.dma_start(out=bias_bc[:, 0, :], in_=upL_b.partition_broadcast(P))
 
         warm = keep.tile([P, 1], F32)
         nc.scalar.activation(out=warm[:], in_=neg_half[:], func=ACT.Silu)
@@ -178,31 +175,6 @@ def tile_mlstmblock_pa_kernel(
         xn_grouped = keep.tile([P, PASSES, P, PACK], BF16, align_bytes=64)
         xn_codes = keep.tile([P, PASSES * P], U32, align_bytes=64)
         xn_scales = keep.tile([P, PASSES * P], U8, align_bytes=64)
-
-        bias_bc = keep.tile([P, 2, WIDTH], BF16)
-
-        spread = {}
-
-        def spread_biases():
-            for half in range(4):
-                side, part = divmod(half, 2)
-                spread[half] = psum.tile([P, HALF], BF16, name="spread", tag="bank%d" % (BANKS + half))
-                for u in range(2):
-                    first = part * HALF + u * BANK
-                    nc.tensor.matmul(
-                        out=spread[half][:, u * BANK : (u + 1) * BANK],
-                        lhsT=ones[:],
-                        rhs=bias_rows[:, side, first : first + BANK],
-                        start=True,
-                        stop=True,
-                    )
-
-        def keep_biases():
-            for half in range(4):
-                side, part = divmod(half, 2)
-                nc.scalar.copy(
-                    out=bias_bc[:, side, part * HALF : (part + 1) * HALF], in_=spread[half][:]
-                )
 
         grouped = {}
         acc = {}
@@ -341,8 +313,6 @@ def tile_mlstmblock_pa_kernel(
                     if (i, step) == (0, 1):
                         norm_out(1)
                         norm_out(3)
-                    if (i, step) == (PASSES - 1, 0):
-                        keep_biases()
                     if (i, step) == (PASSES + 1, 1):
                         keep_leftT(0)
                         keep_leftT(1)
@@ -359,7 +329,7 @@ def tile_mlstmblock_pa_kernel(
                 silu_out(4)
 
             if i == PASSES - 1:
-                left = keep.tile([P, PAD + WIDTH], F32, name="left", tag="early0")
+                left = keep.tile([P, PAD + WIDTH], F32, name="left", tag="left")
                 nc.gpsimd.memset(left[:, 0:PAD], 0.0)
                 conv = keep.tile([P, WIDTH], F32, name="conv", tag="early1")
 
@@ -372,6 +342,8 @@ def tile_mlstmblock_pa_kernel(
                     add_bias(0, step)
             if i < CHUNKS and i + RAW_BUFS < CHUNKS:
                 load_chunk(i + RAW_BUFS)
+                if i + RAW_BUFS == CHUNKS - 1:
+                    nc.sync.dma_start(out=bias_bc[:, 1, :], in_=upR_b.partition_broadcast(P))
             if i == 0:
                 nc.vector.tensor_copy(
                     out=xn_grouped[:], in_=xn_rows[:].rearrange("p c j b -> p c b j")
@@ -388,8 +360,6 @@ def tile_mlstmblock_pa_kernel(
                         in_=xn_grouped[:].rearrange("p c b j -> p (c b j)"),
                     )
                 multiply()
-            if i == 1:
-                spread_biases()
             if i == PASSES:
                 add_bias(0, 2)
                 add_bias(0, 3)

@@ -154,23 +154,13 @@ def tile_mlstmblock_pa_kernel(
         def norm_out(c):
             for j in range(PACK):
                 col = c * PACK + j
-                if c % 2 == 0:
-                    nc.vector.tensor_scalar(
-                        out=xn_rows[:, c, j, :],
-                        in0=zT[c][:, j, :],
-                        scalar1=gain_bf[:, col : col + 1],
-                        scalar2=shift_bf[:, col : col + 1],
-                        op0=ALU.mult,
-                        op1=ALU.add,
-                    )
-                else:
-                    nc.scalar.activation(
-                        out=xn_rows[:, c, j, :],
-                        in_=zT[c][:, j, :],
-                        func=ACT.Identity,
-                        scale=gain[:, col : col + 1],
-                        bias=shift_bf[:, col : col + 1],
-                    )
+                nc.scalar.activation(
+                    out=xn_rows[:, c, j, :],
+                    in_=zT[c][:, j, :],
+                    func=ACT.Identity,
+                    scale=gain[:, col : col + 1],
+                    bias=shift_bf[:, col : col + 1],
+                )
 
         xn_grouped = keep.tile([P, PASSES, P, PACK], BF16, align_bytes=64)
         xn_codes = keep.tile([P, PASSES * P], U32, align_bytes=64)
@@ -311,8 +301,8 @@ def tile_mlstmblock_pa_kernel(
                 for step, (lo, hi) in enumerate(scalar_copies):
                     regroup(nc.scalar.copy, i, lo, hi)
                     if (i, step) == (0, 1):
-                        norm_out(1)
-                        norm_out(3)
+                        for c in range(PASSES):
+                            norm_out(c)
                     if (i, step) == (PASSES + 1, 1):
                         keep_leftT(0)
                         keep_leftT(1)
@@ -335,31 +325,30 @@ def tile_mlstmblock_pa_kernel(
 
             for step, (lo, hi) in enumerate(vector_copies):
                 regroup(nc.vector.tensor_copy, i, lo, hi)
-                if i == 0 and step == 0:
-                    norm_out(0)
-                    norm_out(2)
                 if i == PASSES:
                     add_bias(0, step)
             if i < CHUNKS and i + RAW_BUFS < CHUNKS:
                 load_chunk(i + RAW_BUFS)
                 if i + RAW_BUFS == CHUNKS - 1:
                     nc.sync.dma_start(out=bias_bc[:, 1, :], in_=upR_b.partition_broadcast(P))
-            if i == 0:
+            if i == 1:
                 nc.vector.tensor_copy(
                     out=xn_grouped[:], in_=xn_rows[:].rearrange("p c j b -> p c b j")
                 )
             for h in late:
                 quantise(i - 1, h, pieces=(HALF // BANK if i == CHUNKS else 1))
-                multiply()
-            for h in own:
-                quantise(i, h)
-                if i == 0:
+                if i == 1:
                     nc.vector.quantize_mx(
                         out=xn_codes[:].bitcast(FP8X4),
                         scales=xn_scales[:],
                         in_=xn_grouped[:].rearrange("p c b j -> p (c b j)"),
                     )
-                multiply()
+                if i > 0:
+                    multiply()
+            for h in own:
+                quantise(i, h)
+                if i > 0:
+                    multiply()
             if i == PASSES:
                 add_bias(0, 2)
                 add_bias(0, 3)

@@ -30,7 +30,9 @@ RUN = 8
 EPS = 1e-5
 CHUNKS = 2 * PASSES
 RAW_BUFS = 6
-V_COLS = (1024,) * (CHUNKS - 1) + (1280,)
+V_COLS = (1024, 896, 896, 1024, 1024, 1024, 1024, 1280)
+PE_COLS = (0, 256, 256, 512, 0, 0, 0, 0)
+PE_TILE = 256
 FLOPS = 2 * P * FEATURES * 2 * WIDTH
 
 
@@ -53,6 +55,8 @@ def tile_mlstmblock_pa_kernel(
         nc.gpsimd.memset(neg_half[:], -0.5)
         ident = keep.tile([P, P], F32)
         make_identity(nc, ident[:])
+        ident_bf = keep.tile([P, P], BF16)
+        make_identity(nc, ident_bf[:])
 
         x_sb = keep.tile([P, FEATURES], BF16)
         for h in range(2):
@@ -72,12 +76,13 @@ def tile_mlstmblock_pa_kernel(
 
         def raw_cols(i, lo, hi):
             if i == 0:
-                h = lo // HALF
-                return raw[i][:, h, :, lo - h * HALF : hi - h * HALF]
+                nb = lo // BANK
+                return raw[i][:, nb, :, lo - nb * BANK : hi - nb * BANK]
             return raw[i][:, :, lo:hi]
 
-        raw[0] = raw_pool.tile([P, 2, PACK, HALF], BF16, name="raw", tag="raw")
-        load_rows(0, raw[0][:, 1], HALF, WIDTH)
+        raw[0] = raw_pool.tile([P, BANKS, PACK, BANK], BF16, name="raw", tag="raw")
+        load_rows(0, raw[0][:, 2], 2 * BANK, 3 * BANK)
+        load_rows(0, raw[0][:, 3], 3 * BANK, 4 * BANK)
         gain_bf = keep.tile([P, PASSES * PACK], BF16)
         shift_bf = keep.tile([P, PASSES * PACK], BF16)
         taps_bf = keep.tile([P, TAPS], BF16)
@@ -93,7 +98,8 @@ def tile_mlstmblock_pa_kernel(
             )
             nc.sync.dma_start(out=taps_bf[:], in_=conv_w.partition_broadcast(P))
             nc.sync.dma_start(out=conv_b_bf[:], in_=conv_b.partition_broadcast(P))
-        load_rows(0, raw[0][:, 0], 0, HALF)
+        load_rows(0, raw[0][:, 0], 0, BANK)
+        load_rows(0, raw[0][:, 1], BANK, 2 * BANK)
         bias_bc = keep.tile([P, 2, WIDTH], BF16)
         for i in range(1, RAW_BUFS):
             load_chunk(i)
@@ -177,6 +183,28 @@ def tile_mlstmblock_pa_kernel(
                     "p (q i) j -> p q j i", i=RUN
                 ),
                 in_=raw_cols(i, lo, hi).rearrange("p j (q i) -> p q j i", i=RUN),
+            )
+
+        zipped = []
+
+        def zip_on_tensor(i, lo):
+            tile = psum.tile([P, HALF], BF16, name="zipped", tag="bank%d" % (BANKS + len(zipped)))
+            zipped.append(tile)
+            for v in range(2):
+                first = lo + v * P
+                nc.tensor.matmul(
+                    out=tile[:, v * BANK : (v + 1) * BANK],
+                    lhsT=ident_bf[:],
+                    rhs=raw_cols(i, first, first + P).rearrange("p j n -> p n j"),
+                    start=True,
+                    stop=True,
+                )
+            return tile
+
+        def keep_zipped(i, lo, tile):
+            nc.scalar.copy(
+                out=grouped[i, 1][:, lo - HALF : lo - HALF + PE_TILE, :].rearrange("p n j -> p (n j)"),
+                in_=tile[:],
             )
 
         def quantise(i, h, pieces=1):
@@ -274,6 +302,7 @@ def tile_mlstmblock_pa_kernel(
                 cols = slice((g - 1) * BANK, g * BANK)
                 nc.scalar.dma_start(out=out_1[:, cols], in_=conv[:, cols])
 
+        next_tiles = []
         lagging = []
         for i in range(CHUNKS + 1):
             late = lagging
@@ -296,8 +325,11 @@ def tile_mlstmblock_pa_kernel(
                         lo, hi = nb * BANK, (nb + 1) * BANK
                         if lo < cut:
                             vector_copies.append((lo, min(hi, cut)))
-                        if hi > cut:
-                            scalar_copies.append((max(lo, cut), hi))
+                        if min(hi, WIDTH - PE_COLS[i]) > max(lo, cut):
+                            scalar_copies.append((max(lo, cut), min(hi, WIDTH - PE_COLS[i])))
+                scalar_copies = [s for s in scalar_copies if s[0] >= HALF] + [
+                    s for s in scalar_copies if s[0] < HALF
+                ]
                 for step, (lo, hi) in enumerate(scalar_copies):
                     regroup(nc.scalar.copy, i, lo, hi)
                     if (i, step) == (0, 1):
@@ -315,6 +347,15 @@ def tile_mlstmblock_pa_kernel(
                         keep_leftT(4)
                         silu_out(2)
                         silu_out(3)
+            if i < CHUNKS:
+                for lo, tile in next_tiles:
+                    keep_zipped(i, lo, tile)
+                next_tiles = []
+                if i + 1 < CHUNKS:
+                    next_tiles = [
+                        (lo, zip_on_tensor(i + 1, lo))
+                        for lo in range(WIDTH - PE_COLS[i + 1], WIDTH, PE_TILE)
+                    ]
             if i == CHUNKS:
                 silu_out(4)
 

@@ -262,9 +262,9 @@ def tile_mlstmblock_pa_kernel(
         def windows_of(g):
             return range(g * WINDOWS_PER_BANK, min((g + 1) * WINDOWS_PER_BANK, WINDOWS))
 
-        def turn_left(g):
+        def turn_left(g, bank):
             leftT_ps[g] = psum.tile(
-                [P, WINDOWS_PER_BANK, P], F32, name="leftT_ps", tag="bank%d" % (g % 2)
+                [P, WINDOWS_PER_BANK, P], F32, name="leftT_ps", tag="bank%d" % bank
             )
             for q, w in enumerate(windows_of(g)):
                 first = min(w * STEP, WIDTH - STEP) + PAD - (TAPS - 1)
@@ -276,8 +276,8 @@ def tile_mlstmblock_pa_kernel(
             ws = windows_of(g)
             nc.scalar.copy(out=leftT[:, ws.start : ws.stop, :], in_=leftT_ps[g][:, 0 : len(ws), :])
 
-        def convolve(g):
-            conv_ps[g] = psum.tile([P, BANK], F32, name="conv_ps", tag="bank%d" % (2 + g % 2))
+        def convolve(g, bank):
+            conv_ps[g] = psum.tile([P, BANK], F32, name="conv_ps", tag="bank%d" % bank)
             for q, w in enumerate(windows_of(g)):
                 skip = w * STEP - min(w * STEP, WIDTH - STEP)
                 nc.tensor.matmul(
@@ -327,6 +327,12 @@ def tile_mlstmblock_pa_kernel(
                             vector_copies.append((lo, min(hi, cut)))
                         if min(hi, WIDTH - PE_COLS[i]) > max(lo, cut):
                             scalar_copies.append((max(lo, cut), min(hi, WIDTH - PE_COLS[i])))
+                regroup(nc.vector.tensor_copy, i, *vector_copies[0])
+                if i == PASSES:
+                    add_bias(0, 0)
+                    add_bias(0, 1)
+                    turn_left(0, 0)
+                    turn_left(1, 1)
                 scalar_copies = [s for s in scalar_copies if s[0] >= HALF] + [
                     s for s in scalar_copies if s[0] < HALF
                 ]
@@ -335,18 +341,24 @@ def tile_mlstmblock_pa_kernel(
                     if (i, step) == (0, 1):
                         for c in range(PASSES):
                             norm_out(c)
-                    if (i, step) == (PASSES + 1, 1):
-                        keep_leftT(0)
-                        keep_leftT(1)
-                    if (i, step) == (PASSES + 2, 1):
-                        keep_leftT(2)
-                        keep_leftT(3)
-                        silu_out(0)
-                        silu_out(1)
-                    if (i, step) == (PASSES + 3, 1):
+                    if (i, step) == (PASSES + 1, 0):
+                        for g in range(4):
+                            keep_leftT(g)
+                        turn_left(4, 0)
+                        convolve(0, 1)
+                        convolve(1, 2)
+                        convolve(2, 3)
+                    if (i, step) == (PASSES + 2, 0):
                         keep_leftT(4)
+                        silu_out(0)
+                        convolve(4, 0)
+                        convolve(3, 1)
+                    if (i, step) == (PASSES + 3, 0):
+                        silu_out(1)
                         silu_out(2)
+                    if (i, step) == (PASSES + 3, 1):
                         silu_out(3)
+                        silu_out(4)
             if i < CHUNKS:
                 for lo, tile in next_tiles:
                     keep_zipped(i, lo, tile)
@@ -356,18 +368,24 @@ def tile_mlstmblock_pa_kernel(
                         (lo, zip_on_tensor(i + 1, lo))
                         for lo in range(WIDTH - PE_COLS[i + 1], WIDTH, PE_TILE)
                     ]
-            if i == CHUNKS:
-                silu_out(4)
 
             if i == PASSES - 1:
                 left = keep.tile([P, PAD + WIDTH], F32, name="left", tag="left")
                 nc.gpsimd.memset(left[:, 0:PAD], 0.0)
                 conv = keep.tile([P, WIDTH], F32, name="conv", tag="early1")
 
-            for step, (lo, hi) in enumerate(vector_copies):
+            if i == PASSES:
+                for h in late:
+                    quantise(i - 1, h)
+                    multiply()
+                late = []
+            for lo, hi in vector_copies[1:]:
                 regroup(nc.vector.tensor_copy, i, lo, hi)
-                if i == PASSES:
-                    add_bias(0, step)
+            if i == PASSES:
+                add_bias(0, 2)
+                add_bias(0, 3)
+                turn_left(2, 2)
+                turn_left(3, 3)
             if i < CHUNKS and i + RAW_BUFS < CHUNKS:
                 load_chunk(i + RAW_BUFS)
                 if i + RAW_BUFS == CHUNKS - 1:
@@ -390,22 +408,6 @@ def tile_mlstmblock_pa_kernel(
                 quantise(i, h)
                 if i > 0:
                     multiply()
-            if i == PASSES:
-                add_bias(0, 2)
-                add_bias(0, 3)
-                turn_left(0)
-                turn_left(1)
-            if i == PASSES + 1:
-                turn_left(2)
-                turn_left(3)
-                convolve(0)
-                convolve(1)
-            if i == PASSES + 2:
-                turn_left(4)
-                convolve(2)
-                convolve(3)
-            if i == PASSES + 3:
-                convolve(4)
             if i == CHUNKS:
                 add_bias(1, 2)
                 add_bias(1, 3)

@@ -58,6 +58,21 @@ def tile_mlstmblock_pa_kernel(
         ident_bf = keep.tile([P, P], BF16)
         make_identity(nc, ident_bf[:])
 
+        gain_bf = keep.tile([P, PASSES * PACK], BF16)
+        shift_bf = keep.tile([P, PASSES * PACK], BF16)
+        taps_bf = keep.tile([P, TAPS], BF16)
+        conv_b_bf = keep.tile([P, 1], BF16)
+        with nc.allow_non_contiguous_dma(reason="two vectors of 2048 values, four to a piece"):
+            nc.scalar.dma_start(
+                out=gain_bf[:].rearrange("p (c j) -> p c j", j=PACK),
+                in_=ln_w.rearrange("(c p j) -> p c j", c=PASSES, j=PACK),
+            )
+            nc.scalar.dma_start(
+                out=shift_bf[:].rearrange("p (c j) -> p c j", j=PACK),
+                in_=ln_b.rearrange("(c p j) -> p c j", c=PASSES, j=PACK),
+            )
+            nc.scalar.dma_start(out=taps_bf[:], in_=conv_w.partition_broadcast(P))
+            nc.scalar.dma_start(out=conv_b_bf[:], in_=conv_b.partition_broadcast(P))
         x_sb = keep.tile([P, FEATURES], BF16)
         for h in range(2):
             cols = slice(h * FEATURES // 2, (h + 1) * FEATURES // 2)
@@ -83,21 +98,6 @@ def tile_mlstmblock_pa_kernel(
         raw[0] = raw_pool.tile([P, BANKS, PACK, BANK], BF16, name="raw", tag="raw")
         load_rows(0, raw[0][:, 2], 2 * BANK, 3 * BANK)
         load_rows(0, raw[0][:, 3], 3 * BANK, 4 * BANK)
-        gain_bf = keep.tile([P, PASSES * PACK], BF16)
-        shift_bf = keep.tile([P, PASSES * PACK], BF16)
-        taps_bf = keep.tile([P, TAPS], BF16)
-        conv_b_bf = keep.tile([P, 1], BF16)
-        with nc.allow_non_contiguous_dma(reason="two vectors of 2048 values, four to a piece"):
-            nc.sync.dma_start(
-                out=gain_bf[:].rearrange("p (c j) -> p c j", j=PACK),
-                in_=ln_w.rearrange("(c p j) -> p c j", c=PASSES, j=PACK),
-            )
-            nc.sync.dma_start(
-                out=shift_bf[:].rearrange("p (c j) -> p c j", j=PACK),
-                in_=ln_b.rearrange("(c p j) -> p c j", c=PASSES, j=PACK),
-            )
-            nc.sync.dma_start(out=taps_bf[:], in_=conv_w.partition_broadcast(P))
-            nc.sync.dma_start(out=conv_b_bf[:], in_=conv_b.partition_broadcast(P))
         load_rows(0, raw[0][:, 0], 0, BANK)
         load_rows(0, raw[0][:, 1], BANK, 2 * BANK)
         bias_bc = keep.tile([P, 2, WIDTH], BF16)

@@ -302,6 +302,15 @@ def tile_mlstmblock_pa_kernel(
                 cols = slice((g - 1) * BANK, g * BANK)
                 nc.scalar.dma_start(out=out_1[:, cols], in_=conv[:, cols])
 
+        def joined(pieces):
+            out = []
+            for lo, hi in pieces:
+                if out and out[-1][1] == lo and lo % HALF != 0:
+                    out[-1] = (out[-1][0], hi)
+                else:
+                    out.append((lo, hi))
+            return out
+
         next_tiles = []
         lagging = []
         for i in range(CHUNKS + 1):
@@ -327,6 +336,10 @@ def tile_mlstmblock_pa_kernel(
                             vector_copies.append((lo, min(hi, cut)))
                         if min(hi, WIDTH - PE_COLS[i]) > max(lo, cut):
                             scalar_copies.append((max(lo, cut), min(hi, WIDTH - PE_COLS[i])))
+                if i > 0:
+                    vector_copies = joined(vector_copies)
+                if 0 < i <= PASSES:
+                    scalar_copies = joined(scalar_copies)
                 regroup(nc.vector.tensor_copy, i, *vector_copies[0])
                 if i == PASSES:
                     add_bias(0, 0)
@@ -379,6 +392,10 @@ def tile_mlstmblock_pa_kernel(
                     quantise(i - 1, h)
                     multiply()
                 late = []
+                for h in own:
+                    quantise(i, h)
+                    multiply()
+                own = []
             for lo, hi in vector_copies[1:]:
                 regroup(nc.vector.tensor_copy, i, lo, hi)
             if i == PASSES:

@@ -103,7 +103,7 @@ def tile_mlstmblock_pa_kernel(
         bias_bc = keep.tile([P, 2, WIDTH], BF16)
         for i in range(1, RAW_BUFS):
             load_chunk(i)
-            if i == PASSES - 1:
+            if i == PASSES:
                 nc.sync.dma_start(out=bias_bc[:, 0, :], in_=upL_b.partition_broadcast(P))
 
         warm = keep.tile([P, 1], F32)

@@ -103,7 +103,7 @@ def tile_mlstmblock_pa_kernel(
         bias_bc = keep.tile([P, 2, WIDTH], BF16)
         for i in range(1, RAW_BUFS):
             load_chunk(i)
-            if i == PASSES:
+            if i == PASSES + 1:
                 nc.sync.dma_start(out=bias_bc[:, 0, :], in_=upL_b.partition_broadcast(P))
 
         warm = keep.tile([P, 1], F32)
@@ -341,11 +341,6 @@ def tile_mlstmblock_pa_kernel(
                 if 0 < i <= PASSES:
                     scalar_copies = joined(scalar_copies)
                 regroup(nc.vector.tensor_copy, i, *vector_copies[0])
-                if i == PASSES:
-                    add_bias(0, 0)
-                    add_bias(0, 1)
-                    turn_left(0, 0)
-                    turn_left(1, 1)
                 scalar_copies = [s for s in scalar_copies if s[0] >= HALF] + [
                     s for s in scalar_copies if s[0] < HALF
                 ]
@@ -354,7 +349,7 @@ def tile_mlstmblock_pa_kernel(
                     if (i, step) == (0, 1):
                         for c in range(PASSES):
                             norm_out(c)
-                    if (i, step) == (PASSES + 1, 0):
+                    if (i, step) == (PASSES + 1, 1):
                         for g in range(4):
                             keep_leftT(g)
                         turn_left(4, 0)
@@ -399,10 +394,9 @@ def tile_mlstmblock_pa_kernel(
             for lo, hi in vector_copies[1:]:
                 regroup(nc.vector.tensor_copy, i, lo, hi)
             if i == PASSES:
-                add_bias(0, 2)
-                add_bias(0, 3)
-                turn_left(2, 2)
-                turn_left(3, 3)
+                for g in range(BANKS):
+                    add_bias(0, g)
+                    turn_left(g, g)
             if i < CHUNKS and i + RAW_BUFS < CHUNKS:
                 load_chunk(i + RAW_BUFS)
                 if i + RAW_BUFS == CHUNKS - 1:

@@ -346,7 +346,7 @@ def tile_mlstmblock_pa_kernel(
                 ]
                 for step, (lo, hi) in enumerate(scalar_copies):
                     regroup(nc.scalar.copy, i, lo, hi)
-                    if (i, step) == (0, 1):
+                    if (i, step) == (0, 0):
                         for c in range(PASSES):
                             norm_out(c)
                     if (i, step) == (PASSES + 1, 1):
@@ -401,10 +401,6 @@ def tile_mlstmblock_pa_kernel(
                 load_chunk(i + RAW_BUFS)
                 if i + RAW_BUFS == CHUNKS - 1:
                     nc.sync.dma_start(out=bias_bc[:, 1, :], in_=upR_b.partition_broadcast(P))
-            if i == 1:
-                nc.vector.tensor_copy(
-                    out=xn_grouped[:], in_=xn_rows[:].rearrange("p c j b -> p c b j")
-                )
             for h in late:
                 quantise(i - 1, h, pieces=(HALF // BANK if i == CHUNKS else 1))
                 if i == 1:
@@ -419,6 +415,10 @@ def tile_mlstmblock_pa_kernel(
                 quantise(i, h)
                 if i > 0:
                     multiply()
+            if i == 0:
+                nc.vector.tensor_copy(
+                    out=xn_grouped[:], in_=xn_rows[:].rearrange("p c j b -> p c b j")
+                )
             if i == CHUNKS:
                 add_bias(1, 2)
                 add_bias(1, 3)

@@ -103,7 +103,7 @@ def tile_mlstmblock_pa_kernel(
         bias_bc = keep.tile([P, 2, WIDTH], BF16)
         for i in range(1, RAW_BUFS):
             load_chunk(i)
-            if i == PASSES + 1:
+            if i == PASSES:
                 nc.sync.dma_start(out=bias_bc[:, 0, :], in_=upL_b.partition_broadcast(P))
 
         warm = keep.tile([P, 1], F32)
@@ -340,6 +340,14 @@ def tile_mlstmblock_pa_kernel(
                     vector_copies = joined(vector_copies)
                 if 0 < i <= PASSES:
                     scalar_copies = joined(scalar_copies)
+                if i == PASSES:
+                    for h in late:
+                        quantise(i - 1, h)
+                        multiply()
+                    late = []
+                    for g in range(BANKS):
+                        add_bias(0, g)
+                        turn_left(g, g)
                 regroup(nc.vector.tensor_copy, i, *vector_copies[0])
                 scalar_copies = [s for s in scalar_copies if s[0] >= HALF] + [
                     s for s in scalar_copies if s[0] < HALF
@@ -349,14 +357,14 @@ def tile_mlstmblock_pa_kernel(
                     if (i, step) == (0, 0):
                         for c in range(PASSES):
                             norm_out(c)
-                    if (i, step) == (PASSES + 1, 1):
+                    if (i, step) == (PASSES, 0):
                         for g in range(4):
                             keep_leftT(g)
                         turn_left(4, 0)
                         convolve(0, 1)
                         convolve(1, 2)
                         convolve(2, 3)
-                    if (i, step) == (PASSES + 2, 0):
+                    if (i, step) == (PASSES + 1, 0):
                         keep_leftT(4)
                         silu_out(0)
                         convolve(4, 0)
@@ -383,20 +391,12 @@ def tile_mlstmblock_pa_kernel(
                 conv = keep.tile([P, WIDTH], F32, name="conv", tag="early1")
 
             if i == PASSES:
-                for h in late:
-                    quantise(i - 1, h)
-                    multiply()
-                late = []
                 for h in own:
                     quantise(i, h)
                     multiply()
                 own = []
             for lo, hi in vector_copies[1:]:
                 regroup(nc.vector.tensor_copy, i, lo, hi)
-            if i == PASSES:
-                for g in range(BANKS):
-                    add_bias(0, g)
-                    turn_left(g, g)
             if i < CHUNKS and i + RAW_BUFS < CHUNKS:
                 load_chunk(i + RAW_BUFS)
                 if i + RAW_BUFS == CHUNKS - 1:

@@ -369,10 +369,9 @@ def tile_mlstmblock_pa_kernel(
                         silu_out(0)
                         convolve(4, 0)
                         convolve(3, 1)
-                    if (i, step) == (PASSES + 3, 0):
+                    if (i, step) == (PASSES + 3, 1):
                         silu_out(1)
                         silu_out(2)
-                    if (i, step) == (PASSES + 3, 1):
                         silu_out(3)
                         silu_out(4)
             if i < CHUNKS:

@@ -30,7 +30,7 @@ RUN = 8
 EPS = 1e-5
 CHUNKS = 2 * PASSES
 RAW_BUFS = 6
-V_COLS = (1024, 896, 896, 1024, 1024, 1024, 1024, 1280)
+V_COLS = (1024, 896, 896, 1024, 1024, 896, 896, 1280)
 PE_COLS = (0, 256, 256, 512, 0, 0, 0, 0)
 PE_TILE = 256
 FLOPS = 2 * P * FEATURES * 2 * WIDTH

@@ -51,6 +51,8 @@ def tile_mlstmblock_pa_kernel(
         psum = ctx.enter_context(tc.psum_pool(name="psum", bufs=1))
         ctx.enter_context(tc.manual_schedule())
 
+        bias_rows = keep.tile([P, P], BF16)
+        nc.gpsimd.memset(bias_rows[:], 0.0)
         neg_half = keep.tile([P, 1], F32)
         nc.gpsimd.memset(neg_half[:], -0.5)
         ident = keep.tile([P, P], F32)
@@ -62,6 +64,9 @@ def tile_mlstmblock_pa_kernel(
         shift_bf = keep.tile([P, PASSES * PACK], BF16)
         taps_bf = keep.tile([P, TAPS], BF16)
         conv_b_bf = keep.tile([P, 1], BF16)
+        nc.scalar.dma_start(
+            out=bias_rows[0 : WIDTH // P, :], in_=upL_b.rearrange("(r q) -> r q", q=P)
+        )
         with nc.allow_non_contiguous_dma(reason="two vectors of 2048 values, four to a piece"):
             nc.scalar.dma_start(
                 out=gain_bf[:].rearrange("p (c j) -> p c j", j=PACK),
@@ -103,11 +108,24 @@ def tile_mlstmblock_pa_kernel(
         bias_bc = keep.tile([P, 2, WIDTH], BF16)
         for i in range(1, RAW_BUFS):
             load_chunk(i)
-            if i == PASSES:
-                nc.sync.dma_start(out=bias_bc[:, 0, :], in_=upL_b.partition_broadcast(P))
 
         warm = keep.tile([P, 1], F32)
         nc.scalar.activation(out=warm[:], in_=neg_half[:], func=ACT.Silu)
+
+        biasT_ps = psum.tile([P, P], BF16, name="biasT_ps", tag="bank0")
+        nc.tensor.transpose(out=biasT_ps[:], in_=bias_rows[:], identity=ident_bf[:])
+        biasT = keep.tile([P, WIDTH // P], BF16)
+        nc.scalar.copy(out=biasT[:], in_=biasT_ps[:, 0 : WIDTH // P])
+        spread = []
+        for h in range(2):
+            spread.append(psum.tile([P, HALF], BF16, name="spread", tag="bank%d" % (1 + h)))
+            for r in range(HALF // P):
+                col = h * (HALF // P) + r
+                nc.tensor.transpose(
+                    out=spread[h][:, r * P : (r + 1) * P],
+                    in_=biasT[:, col : col + 1].to_broadcast([P, P]),
+                    identity=ident_bf[:],
+                )
 
         stats = keep.tile([P, PASSES, 6], F32)
         for c in range(PASSES):
@@ -355,6 +373,10 @@ def tile_mlstmblock_pa_kernel(
                 for step, (lo, hi) in enumerate(scalar_copies):
                     regroup(nc.scalar.copy, i, lo, hi)
                     if (i, step) == (0, 0):
+                        for h in range(2):
+                            nc.scalar.copy(
+                                out=bias_bc[:, 0, h * HALF : (h + 1) * HALF], in_=spread[h][:]
+                            )
                         for c in range(PASSES):
                             norm_out(c)
                     if (i, step) == (PASSES, 0):

@@ -33,6 +33,7 @@ RAW_BUFS = 6
 V_COLS = (1024, 896, 896, 1024, 1024, 896, 896, 1280)
 PE_COLS = (0, 256, 256, 512, 0, 0, 0, 0)
 PE_TILE = 256
+G_COLS = 320
 FLOPS = 2 * P * FEATURES * 2 * WIDTH
 
 
@@ -53,6 +54,8 @@ def tile_mlstmblock_pa_kernel(
 
         bias_rows = keep.tile([P, P], BF16)
         nc.gpsimd.memset(bias_rows[:], 0.0)
+        ln_rows = keep.tile([P, K_PASS], BF16)
+        nc.gpsimd.memset(ln_rows[:], 0.0)
         neg_half = keep.tile([P, 1], F32)
         nc.gpsimd.memset(neg_half[:], -0.5)
         ident = keep.tile([P, P], F32)
@@ -60,22 +63,16 @@ def tile_mlstmblock_pa_kernel(
         ident_bf = keep.tile([P, P], BF16)
         make_identity(nc, ident_bf[:])
 
-        gain_bf = keep.tile([P, PASSES * PACK], BF16)
-        shift_bf = keep.tile([P, PASSES * PACK], BF16)
         taps_bf = keep.tile([P, TAPS], BF16)
         conv_b_bf = keep.tile([P, 1], BF16)
         nc.scalar.dma_start(
             out=bias_rows[0 : WIDTH // P, :], in_=upL_b.rearrange("(r q) -> r q", q=P)
         )
-        with nc.allow_non_contiguous_dma(reason="two vectors of 2048 values, four to a piece"):
-            nc.scalar.dma_start(
-                out=gain_bf[:].rearrange("p (c j) -> p c j", j=PACK),
-                in_=ln_w.rearrange("(c p j) -> p c j", c=PASSES, j=PACK),
-            )
-            nc.scalar.dma_start(
-                out=shift_bf[:].rearrange("p (c j) -> p c j", j=PACK),
-                in_=ln_b.rearrange("(c p j) -> p c j", c=PASSES, j=PACK),
-            )
+        nc.scalar.dma_start(out=ln_rows[0:PASSES, :], in_=ln_w.rearrange("(c k) -> c k", k=K_PASS))
+        nc.scalar.dma_start(
+            out=ln_rows[PASSES : 2 * PASSES, :], in_=ln_b.rearrange("(c k) -> c k", k=K_PASS)
+        )
+        with nc.allow_non_contiguous_dma(reason="five values for every partition"):
             nc.scalar.dma_start(out=taps_bf[:], in_=conv_w.partition_broadcast(P))
             nc.scalar.dma_start(out=conv_b_bf[:], in_=conv_b.partition_broadcast(P))
         x_sb = keep.tile([P, FEATURES], BF16)
@@ -127,6 +124,14 @@ def tile_mlstmblock_pa_kernel(
                     identity=ident_bf[:],
                 )
 
+        lnT_ps = psum.tile([P, PACK, P], BF16, name="lnT_ps", tag="bank3")
+        for j in range(PACK):
+            nc.tensor.transpose(
+                out=lnT_ps[:, j, :], in_=ln_rows[:, j : K_PASS : PACK], identity=ident_bf[:]
+            )
+        gain = keep.tile([P, PASSES * PACK], F32)
+        shift = keep.tile([P, PASSES * PACK], F32)
+
         stats = keep.tile([P, PASSES, 6], F32)
         for c in range(PASSES):
             nc.vector.bn_stats(out=stats[:, c, :], in_=x_sb[:, c * K_PASS : (c + 1) * K_PASS])
@@ -139,8 +144,6 @@ def tile_mlstmblock_pa_kernel(
         rstd = keep.tile([P, 1], F32)
         nc.gpsimd.tensor_tensor(out=rstd[:], in0=var_eps[:], in1=neg_half[:], op=ALU.pow)
 
-        gain = keep.tile([P, PASSES * PACK], F32)
-        nc.gpsimd.tensor_copy(out=gain[:], in_=gain_bf[:])
         conv_bias = keep.tile([P, 1], F32)
         nc.gpsimd.tensor_copy(out=conv_bias[:], in_=conv_b_bf[:])
         band = keep.tile([P, STEP], F32)
@@ -183,7 +186,7 @@ def tile_mlstmblock_pa_kernel(
                     in_=zT[c][:, j, :],
                     func=ACT.Identity,
                     scale=gain[:, col : col + 1],
-                    bias=shift_bf[:, col : col + 1],
+                    bias=shift[:, col : col + 1],
                 )
 
         xn_grouped = keep.tile([P, PASSES, P, PACK], BF16, align_bytes=64)
@@ -329,6 +332,7 @@ def tile_mlstmblock_pa_kernel(
                     out.append((lo, hi))
             return out
 
+        go = keep.tile([P, 1], F32)
         next_tiles = []
         lagging = []
         for i in range(CHUNKS + 1):
@@ -363,6 +367,16 @@ def tile_mlstmblock_pa_kernel(
                         quantise(i - 1, h)
                         multiply()
                     late = []
+                    nc.vector.memset(go[:], 1.0)
+                    nc.gpsimd.tensor_scalar(
+                        out=grouped[i, 1][:, HALF - G_COLS : HALF, :],
+                        in0=raw_cols(i, WIDTH - G_COLS, WIDTH).rearrange("p j n -> p n j"),
+                        scalar1=go[:, 0:1],
+                        scalar2=0.0,
+                        op0=ALU.mult,
+                        op1=ALU.add,
+                    )
+                    scalar_copies = [(HALF, WIDTH - G_COLS)]
                     for g in range(BANKS):
                         add_bias(0, g)
                         turn_left(g, g)
@@ -377,6 +391,14 @@ def tile_mlstmblock_pa_kernel(
                             nc.scalar.copy(
                                 out=bias_bc[:, 0, h * HALF : (h + 1) * HALF], in_=spread[h][:]
                             )
+                        nc.scalar.copy(
+                            out=gain[:].rearrange("p (c j) -> p c j", j=PACK),
+                            in_=lnT_ps[:, :, 0:PASSES].rearrange("p j c -> p c j"),
+                        )
+                        nc.scalar.copy(
+                            out=shift[:].rearrange("p (c j) -> p c j", j=PACK),
+                            in_=lnT_ps[:, :, PASSES : 2 * PASSES].rearrange("p j c -> p c j"),
+                        )
                         for c in range(PASSES):
                             norm_out(c)
                     if (i, step) == (PASSES, 0):

from contextlib import ExitStack

import concourse.mybir as mybir
from concourse.masks import make_identity

F32 = mybir.dt.float32
BF16 = mybir.dt.bfloat16
U32 = mybir.dt.uint32
U8 = mybir.dt.uint8
FP8X4 = mybir.dt.float8_e4m3fn_x4
ALU = mybir.AluOpType
ACT = mybir.ActivationFunctionType

P = 128
PACK = 4
K_PASS = P * PACK
FEATURES = 2048
PASSES = FEATURES // K_PASS
WIDTH = 2048
HALF = WIDTH // 2
BANK = 512
BANKS = WIDTH // BANK
BLOCKS_PER_BANK = BANK // P
TAPS = 4
STEP = P - (TAPS - 1)
WINDOWS = -(-WIDTH // STEP)
WINDOWS_PER_BANK = BANK // P
PAD = 8
RUN = 8
EPS = 1e-5
CHUNKS = 2 * PASSES
RAW_BUFS = 6
V_COLS = (1024, 896, 896, 1024, 1024, 896, 896, 1280)
PE_COLS = (0, 256, 256, 512, 0, 0, 0, 0)
PE_TILE = 256
G_COLS = 320
FLOPS = 2 * P * FEATURES * 2 * WIDTH


def tile_mlstmblock_pa_kernel(
    tc, x, ln_w, ln_b, upL_w, upL_b, upR_w, upR_b, conv_w, conv_b, out_0, out_1, out_2
):
    nc = tc.nc
    weights = (upL_w, upR_w)
    outs = (out_0, out_2)
    with ExitStack() as ctx:
        keep = ctx.enter_context(tc.tile_pool(name="keep", bufs=1))
        raw_pool = ctx.enter_context(tc.tile_pool(name="raw", bufs=RAW_BUFS))
        grouped_pool = ctx.enter_context(tc.tile_pool(name="grouped", bufs=6))
        codes_pool = ctx.enter_context(tc.tile_pool(name="codes", bufs=6))
        stage = ctx.enter_context(tc.tile_pool(name="stage", bufs=4))
        psum = ctx.enter_context(tc.psum_pool(name="psum", bufs=1))
        ctx.enter_context(tc.manual_schedule())

        bias_rows = keep.tile([P, P], BF16)
        nc.gpsimd.memset(bias_rows[:], 0.0)
        ln_rows = keep.tile([P, K_PASS], BF16)
        nc.gpsimd.memset(ln_rows[:], 0.0)
        neg_half = keep.tile([P, 1], F32)
        nc.gpsimd.memset(neg_half[:], -0.5)
        ident = keep.tile([P, P], F32)
        make_identity(nc, ident[:])
        ident_bf = keep.tile([P, P], BF16)
        make_identity(nc, ident_bf[:])

        taps_bf = keep.tile([P, TAPS], BF16)
        conv_b_bf = keep.tile([P, 1], BF16)
        nc.scalar.dma_start(
            out=bias_rows[0 : WIDTH // P, :], in_=upL_b.rearrange("(r q) -> r q", q=P)
        )
        nc.scalar.dma_start(out=ln_rows[0:PASSES, :], in_=ln_w.rearrange("(c k) -> c k", k=K_PASS))
        nc.scalar.dma_start(
            out=ln_rows[PASSES : 2 * PASSES, :], in_=ln_b.rearrange("(c k) -> c k", k=K_PASS)
        )
        with nc.allow_non_contiguous_dma(reason="five values for every partition"):
            nc.scalar.dma_start(out=taps_bf[:], in_=conv_w.partition_broadcast(P))
            nc.scalar.dma_start(out=conv_b_bf[:], in_=conv_b.partition_broadcast(P))
        x_sb = keep.tile([P, FEATURES], BF16)
        for h in range(2):
            cols = slice(h * FEATURES // 2, (h + 1) * FEATURES // 2)
            nc.sync.dma_start(out=x_sb[:, cols], in_=x[:, cols])

        raw = {}

        def load_rows(i, out, lo, hi):
            side, c = divmod(i, PASSES)
            rows = weights[side][c * K_PASS : (c + 1) * K_PASS, lo:hi]
            nc.sync.dma_start(out=out, in_=rows.rearrange("(p j) n -> p j n", j=PACK))

        def load_chunk(i):
            raw[i] = raw_pool.tile([P, PACK, WIDTH], BF16, name="raw", tag="raw")
            load_rows(i, raw[i][:], 0, WIDTH)

        def raw_cols(i, lo, hi):
            if i == 0:
                nb = lo // BANK
                return raw[i][:, nb, :, lo - nb * BANK : hi - nb * BANK]
            return raw[i][:, :, lo:hi]

        raw[0] = raw_pool.tile([P, BANKS, PACK, BANK], BF16, name="raw", tag="raw")
        load_rows(0, raw[0][:, 2], 2 * BANK, 3 * BANK)
        load_rows(0, raw[0][:, 3], 3 * BANK, 4 * BANK)
        load_rows(0, raw[0][:, 0], 0, BANK)
        load_rows(0, raw[0][:, 1], BANK, 2 * BANK)
        bias_bc = keep.tile([P, 2, WIDTH], BF16)
        for i in range(1, RAW_BUFS):
            load_chunk(i)

        warm = keep.tile([P, 1], F32)
        nc.scalar.activation(out=warm[:], in_=neg_half[:], func=ACT.Silu)

        biasT_ps = psum.tile([P, P], BF16, name="biasT_ps", tag="bank0")
        nc.tensor.transpose(out=biasT_ps[:], in_=bias_rows[:], identity=ident_bf[:])
        biasT = keep.tile([P, WIDTH // P], BF16)
        nc.scalar.copy(out=biasT[:], in_=biasT_ps[:, 0 : WIDTH // P])
        spread = []
        for h in range(2):
            spread.append(psum.tile([P, HALF], BF16, name="spread", tag="bank%d" % (1 + h)))
            for r in range(HALF // P):
                col = h * (HALF // P) + r
                nc.tensor.transpose(
                    out=spread[h][:, r * P : (r + 1) * P],
                    in_=biasT[:, col : col + 1].to_broadcast([P, P]),
                    identity=ident_bf[:],
                )

        lnT_ps = psum.tile([P, PACK, P], BF16, name="lnT_ps", tag="bank3")
        for j in range(PACK):
            nc.tensor.transpose(
                out=lnT_ps[:, j, :], in_=ln_rows[:, j : K_PASS : PACK], identity=ident_bf[:]
            )
        gain = keep.tile([P, PASSES * PACK], F32)
        shift = keep.tile([P, PASSES * PACK], F32)

        stats = keep.tile([P, PASSES, 6], F32)
        for c in range(PASSES):
            nc.vector.bn_stats(out=stats[:, c, :], in_=x_sb[:, c * K_PASS : (c + 1) * K_PASS])
        mean_var = keep.tile([P, 2], F32)
        nc.vector.bn_aggr(out=mean_var[:], in_=stats[:].rearrange("p c s -> p (c s)"))
        var_eps = keep.tile([P, 1], F32)
        nc.vector.tensor_scalar(
            out=var_eps[:], in0=mean_var[:, 1:2], scalar1=EPS, scalar2=None, op0=ALU.add
        )
        rstd = keep.tile([P, 1], F32)
        nc.gpsimd.tensor_tensor(out=rstd[:], in0=var_eps[:], in1=neg_half[:], op=ALU.pow)

        conv_bias = keep.tile([P, 1], F32)
        nc.gpsimd.tensor_copy(out=conv_bias[:], in_=conv_b_bf[:])
        band = keep.tile([P, STEP], F32)
        nc.vector.tensor_scalar(
            out=band[:], in0=ident[:, 0:STEP], scalar1=taps_bf[:, 0:1], scalar2=None, op0=ALU.mult
        )
        for t in range(1, TAPS):
            nc.vector.scalar_tensor_tensor(
                out=band[:],
                in0=ident[:, t : t + STEP],
                scalar=taps_bf[:, t : t + 1],
                in1=band[:],
                op0=ALU.mult,
                op1=ALU.add,
            )

        z = keep.tile([P, PASSES, PACK, P], F32, name="z", tag="early1")
        x_by_word = x_sb[:].rearrange("b (c p j) -> b c j p", c=PASSES, j=PACK)
        zT = []
        for c in range(PASSES):
            nc.vector.tensor_scalar(
                out=z[:, c],
                in0=x_by_word[:, c],
                scalar1=mean_var[:, 0:1],
                scalar2=rstd[:],
                op0=ALU.subtract,
                op1=ALU.mult,
            )
            zT.append(psum.tile([P, PACK, P], F32, name="zT", tag="bank%d" % (BANKS + c)))
            for j in range(PACK):
                nc.tensor.transpose(out=zT[c][:, j, :], in_=z[:, c, j, :], identity=ident[:])

        xn_rows = keep.tile([P, PASSES, PACK, P], BF16)

        def norm_out(c):
            for j in range(PACK):
                col = c * PACK + j
                nc.scalar.activation(
                    out=xn_rows[:, c, j, :],
                    in_=zT[c][:, j, :],
                    func=ACT.Identity,
                    scale=gain[:, col : col + 1],
                    bias=shift[:, col : col + 1],
                )

        xn_grouped = keep.tile([P, PASSES, P, PACK], BF16, align_bytes=64)
        xn_codes = keep.tile([P, PASSES * P], U32, align_bytes=64)
        xn_scales = keep.tile([P, PASSES * P], U8, align_bytes=64)

        grouped = {}
        acc = {}
        waiting = []

        def regroup(engine_copy, i, lo, hi):
            h = lo // HALF
            engine_copy(
                out=grouped[i, h][:, lo - h * HALF : hi - h * HALF, :].rearrange(
                    "p (q i) j -> p q j i", i=RUN
                ),
                in_=raw_cols(i, lo, hi).rearrange("p j (q i) -> p q j i", i=RUN),
            )

        zipped = []

        def zip_on_tensor(i, lo):
            tile = psum.tile([P, HALF], BF16, name="zipped", tag="bank%d" % (BANKS + len(zipped)))
            zipped.append(tile)
            for v in range(2):
                first = lo + v * P
                nc.tensor.matmul(
                    out=tile[:, v * BANK : (v + 1) * BANK],
                    lhsT=ident_bf[:],
                    rhs=raw_cols(i, first, first + P).rearrange("p j n -> p n j"),
                    start=True,
                    stop=True,
                )
            return tile

        def keep_zipped(i, lo, tile):
            nc.scalar.copy(
                out=grouped[i, 1][:, lo - HALF : lo - HALF + PE_TILE, :].rearrange("p n j -> p (n j)"),
                in_=tile[:],
            )

        def quantise(i, h, pieces=1):
            codes = codes_pool.tile([P, HALF], U32, align_bytes=64, name="codes", tag="codes")
            scales = codes_pool.tile([P, HALF], U8, align_bytes=64, name="scales", tag="scales")
            wide = HALF // pieces
            for u in range(pieces):
                nc.vector.quantize_mx(
                    out=codes[:, u * wide : (u + 1) * wide].bitcast(FP8X4),
                    scales=scales[:, u * wide : (u + 1) * wide],
                    in_=grouped[i, h][:, u * wide : (u + 1) * wide, :].rearrange("p n j -> p (n j)"),
                )
                if pieces > 1:
                    add_bias(1, u)
            for u in range(HALF // BANK):
                waiting.append((i, h * (HALF // BANK) + u, codes, scales, u * BANK))

        def multiply():
            for i, nb, codes, scales, first in waiting:
                side, c = divmod(i, PASSES)
                if c == 0:
                    acc[side, nb] = psum.tile(
                        [P, BANK], F32, name="acc", tag="bank%d" % (side * BANKS + nb)
                    )
                nc.tensor.matmul_mx(
                    out=acc[side, nb][:],
                    lhsT=xn_codes[:, c * P : (c + 1) * P].bitcast(FP8X4),
                    lhsT_scale=xn_scales[:, c * P : (c + 1) * P],
                    rhs=codes[:, first : first + BANK].bitcast(FP8X4),
                    rhs_scale=scales[:, first : first + BANK],
                    start=(c == 0),
                    stop=(c == PASSES - 1),
                )
            waiting.clear()

        left = None
        conv = None

        def add_bias(side, nb):
            cols = slice(nb * BANK, (nb + 1) * BANK)
            if side == 0:
                biased = left[:, PAD + nb * BANK : PAD + (nb + 1) * BANK]
            else:
                staged = stage.tile([P, BANK], F32, name="staged", tag="staged")
                biased = staged[:]
            nc.vector.tensor_tensor(
                out=biased, in0=acc[side, nb][:], in1=bias_bc[:, side, cols], op=ALU.add
            )
            nc.sync.dma_start(out=outs[side][:, cols], in_=biased)

        leftT = keep.tile([P, WINDOWS, P], F32)
        leftT_ps = {}
        conv_ps = {}

        def windows_of(g):
            return range(g * WINDOWS_PER_BANK, min((g + 1) * WINDOWS_PER_BANK, WINDOWS))

        def turn_left(g, bank):
            leftT_ps[g] = psum.tile(
                [P, WINDOWS_PER_BANK, P], F32, name="leftT_ps", tag="bank%d" % bank
            )
            for q, w in enumerate(windows_of(g)):
                first = min(w * STEP, WIDTH - STEP) + PAD - (TAPS - 1)
                nc.tensor.transpose(
                    out=leftT_ps[g][:, q, :], in_=left[:, first : first + P], identity=ident[:]
                )

        def keep_leftT(g):
            ws = windows_of(g)
            nc.scalar.copy(out=leftT[:, ws.start : ws.stop, :], in_=leftT_ps[g][:, 0 : len(ws), :])

        def convolve(g, bank):
            conv_ps[g] = psum.tile([P, BANK], F32, name="conv_ps", tag="bank%d" % bank)
            for q, w in enumerate(windows_of(g)):
                skip = w * STEP - min(w * STEP, WIDTH - STEP)
                nc.tensor.matmul(
                    out=conv_ps[g][:, q * STEP : (q + 1) * STEP - skip],
                    lhsT=leftT[:, w, :],
                    rhs=band[:, skip:STEP],
                    start=True,
                    stop=True,
                )

        def silu_out(g):
            first = g * WINDOWS_PER_BANK * STEP
            last = min(first + WINDOWS_PER_BANK * STEP, WIDTH)
            nc.scalar.activation(
                out=conv[:, first:last],
                in_=conv_ps[g][:, 0 : last - first],
                func=ACT.Silu,
                bias=conv_bias[:],
                scale=1.0,
            )
            if g > 0:
                cols = slice((g - 1) * BANK, g * BANK)
                nc.scalar.dma_start(out=out_1[:, cols], in_=conv[:, cols])

        def joined(pieces):
            out = []
            for lo, hi in pieces:
                if out and out[-1][1] == lo and lo % HALF != 0:
                    out[-1] = (out[-1][0], hi)
                else:
                    out.append((lo, hi))
            return out

        go = keep.tile([P, 1], F32)
        next_tiles = []
        lagging = []
        for i in range(CHUNKS + 1):
            late = lagging
            lagging = []
            own = []
            vector_copies = []
            if i < CHUNKS:
                cut = V_COLS[i]
                scalar_copies = []
                for h in range(2):
                    lo, hi = h * HALF, (h + 1) * HALF
                    grouped[i, h] = grouped_pool.tile(
                        [P, HALF, PACK], BF16, align_bytes=64, name="grouped", tag="grouped"
                    )
                    if hi <= cut:
                        own.append(h)
                    else:
                        lagging.append(h)
                    for nb in (2 * h, 2 * h + 1):
                        lo, hi = nb * BANK, (nb + 1) * BANK
                        if lo < cut:
                            vector_copies.append((lo, min(hi, cut)))
                        if min(hi, WIDTH - PE_COLS[i]) > max(lo, cut):
                            scalar_copies.append((max(lo, cut), min(hi, WIDTH - PE_COLS[i])))
                if i > 0:
                    vector_copies = joined(vector_copies)
                if 0 < i <= PASSES:
                    scalar_copies = joined(scalar_copies)
                if i == PASSES:
                    for h in late:
                        quantise(i - 1, h)
                        multiply()
                    late = []
                    nc.vector.memset(go[:], 1.0)
                    nc.gpsimd.tensor_scalar(
                        out=grouped[i, 1][:, HALF - G_COLS : HALF, :],
                        in0=raw_cols(i, WIDTH - G_COLS, WIDTH).rearrange("p j n -> p n j"),
                        scalar1=go[:, 0:1],
                        scalar2=0.0,
                        op0=ALU.mult,
                        op1=ALU.add,
                    )
                    scalar_copies = [(HALF, WIDTH - G_COLS)]
                    for g in range(BANKS):
                        add_bias(0, g)
                        turn_left(g, g)
                regroup(nc.vector.tensor_copy, i, *vector_copies[0])
                scalar_copies = [s for s in scalar_copies if s[0] >= HALF] + [
                    s for s in scalar_copies if s[0] < HALF
                ]
                for step, (lo, hi) in enumerate(scalar_copies):
                    regroup(nc.scalar.copy, i, lo, hi)
                    if (i, step) == (0, 0):
                        for h in range(2):
                            nc.scalar.copy(
                                out=bias_bc[:, 0, h * HALF : (h + 1) * HALF], in_=spread[h][:]
                            )
                        nc.scalar.copy(
                            out=gain[:].rearrange("p (c j) -> p c j", j=PACK),
                            in_=lnT_ps[:, :, 0:PASSES].rearrange("p j c -> p c j"),
                        )
                        nc.scalar.copy(
                            out=shift[:].rearrange("p (c j) -> p c j", j=PACK),
                            in_=lnT_ps[:, :, PASSES : 2 * PASSES].rearrange("p j c -> p c j"),
                        )
                        for c in range(PASSES):
                            norm_out(c)
                    if (i, step) == (PASSES, 0):
                        for g in range(4):
                            keep_leftT(g)
                        turn_left(4, 0)
                        convolve(0, 1)
                        convolve(1, 2)
                        convolve(2, 3)
                    if (i, step) == (PASSES + 1, 0):
                        keep_leftT(4)
                        silu_out(0)
                        convolve(4, 0)
                        convolve(3, 1)
                    if (i, step) == (PASSES + 3, 1):
                        silu_out(1)
                        silu_out(2)
                        silu_out(3)
                        silu_out(4)
            if i < CHUNKS:
                for lo, tile in next_tiles:
                    keep_zipped(i, lo, tile)
                next_tiles = []
                if i + 1 < CHUNKS:
                    next_tiles = [
                        (lo, zip_on_tensor(i + 1, lo))
                        for lo in range(WIDTH - PE_COLS[i + 1], WIDTH, PE_TILE)
                    ]

            if i == PASSES - 1:
                left = keep.tile([P, PAD + WIDTH], F32, name="left", tag="left")
                nc.gpsimd.memset(left[:, 0:PAD], 0.0)
                conv = keep.tile([P, WIDTH], F32, name="conv", tag="early1")

            if i == PASSES:
                for h in own:
                    quantise(i, h)
                    multiply()
                own = []
            for lo, hi in vector_copies[1:]:
                regroup(nc.vector.tensor_copy, i, lo, hi)
            if i < CHUNKS and i + RAW_BUFS < CHUNKS:
                load_chunk(i + RAW_BUFS)
                if i + RAW_BUFS == CHUNKS - 1:
                    nc.sync.dma_start(out=bias_bc[:, 1, :], in_=upR_b.partition_broadcast(P))
            for h in late:
                quantise(i - 1, h, pieces=(HALF // BANK if i == CHUNKS else 1))
                if i == 1:
                    nc.vector.quantize_mx(
                        out=xn_codes[:].bitcast(FP8X4),
                        scales=xn_scales[:],
                        in_=xn_grouped[:].rearrange("p c b j -> p (c b j)"),
                    )
                if i > 0:
                    multiply()
            for h in own:
                quantise(i, h)
                if i > 0:
                    multiply()
            if i == 0:
                nc.vector.tensor_copy(
                    out=xn_grouped[:], in_=xn_rows[:].rearrange("p c j b -> p c b j")
                )
            if i == CHUNKS:
                add_bias(1, 2)
                add_bias(1, 3)
